import numpy as np
import ml_dtypes


def mxq(x, axis, fmt="e4m3"):
    dtype, down = {"e4m3": (ml_dtypes.float8_e4m3fn, 7), "e5m2": (ml_dtypes.float8_e5m2, 14)}[fmt]
    v = np.moveaxis(np.asarray(x, np.float32).astype(ml_dtypes.bfloat16).astype(np.float64), axis, -1)
    blocks = v.reshape(v.shape[:-1] + (-1, 32))
    amax = np.abs(blocks).max(-1, keepdims=True)
    byte = np.maximum(np.where(amax > 0, np.frexp(amax)[1] - 1 + 127, 0) - down, 1)
    scale = np.exp2(byte - 127.0)
    codes = (blocks / scale).astype(np.float32).astype(dtype).astype(np.float64)
    return np.moveaxis((codes * scale).reshape(v.shape), -1, axis)


WIDE = False


def mx_kscale(k):
    if not WIDE:
        return np.ones(k)
    levels = np.array([10, -10, 5, -5, 0])
    if k % 512:
        return np.exp2(np.random.permutation(np.resize(levels, k // 32))).repeat(32)
    a = np.empty((k // 512, 16))
    for p in range(k // 512):
        a[p, :8] = np.random.permutation(np.resize(levels, 8))
        for g in range(8):
            far = levels[np.abs(levels - a[p, g]) >= 10]
            a[p, g + 8] = far[np.random.randint(len(far))]
    return np.exp2(a.ravel()).repeat(32)


BF16 = ml_dtypes.bfloat16


def bf(x):
    return np.asarray(x, np.float32).astype(BF16)


def f64(x):
    return np.asarray(x).astype(np.float64)


BS, CIN, H, D, L, P, OUT_DIM = 8, 512, 256, 1024, 10, 2, 128
K0, K1 = CIN * P, H * P


def patch_conv_relu(y, w):
    bs, cin, d = y.shape
    out, p = w.shape[0], w.shape[-1]
    q = d // p
    rows = y.reshape(bs, cin, q, p).transpose(0, 2, 1, 3).reshape(bs * q, cin * p)
    wm = w.reshape(out, cin * p).T
    z = (mxq(rows, 1, "e4m3") @ mxq(wm, 0, "e4m3")) * (1.0 / np.sqrt(cin))
    return np.maximum(z, 0.0).reshape(bs, q, out).transpose(0, 2, 1)


def draw0():
    s = mx_kscale(K0).reshape(CIN, P)
    t = mx_kscale(K1)[::P]
    return {"x": bf(np.random.standard_normal((BS, CIN, D)) * np.tile(s, (1, D // P))),
            "w0": bf(np.random.standard_normal((H, CIN, P)) / s * t[:, None, None]),
            "w1": bf(np.random.standard_normal((H, H, P)) / t[:, None])}


def core(x, w0, w1):
    h = patch_conv_relu(f64(x), f64(w0))
    return patch_conv_relu(h, f64(w1))


def e4m3fn_bytes(y):
    return np.clip(np.asarray(y, np.float64), -448.0, 448.0).astype(np.float32).astype(ml_dtypes.float8_e4m3fn).view(np.uint8)


def e4m3fn_values(b):
    return np.asarray(b, np.uint8).view(ml_dtypes.float8_e4m3fn).astype(np.float64)


def setup_inputs():
    d = draw0()
    x0 = np.asarray(d['x']).astype(np.float64)
    s = (np.max(np.abs(x0), axis=(0, 2), keepdims=True) / 448.0).astype(np.float32)
    out = {}
    for k, v in d.items():
        if k == 'x':
            out['x_bytes'] = e4m3fn_bytes(x0 / s.astype(np.float64))
            out['x_scale'] = s
        else:
            out[k] = v
    return out


def reference(x_bytes, x_scale, w0, w1):
    return core(e4m3fn_values(x_bytes) * x_scale.astype(np.float64), w0, w1)

@@ -1,0 +1,262 @@
+import math
+from contextlib import ExitStack
+
+import concourse.mybir as mybir
+from concourse.masks import make_identity
+
+BS, CIN, HID, D, OUT_DIM = 8, 512, 256, 1024, 256
+P = 128
+Q = D // 2
+R = Q // 2
+G = 2
+HALF = Q // 2
+
+FLOPS = 2 * BS * Q * HID * (2 * CIN) + 2 * BS * R * OUT_DIM * (2 * HID)
+
+F32 = mybir.dt.float32
+BF16 = mybir.dt.bfloat16
+U32 = mybir.dt.uint32
+U8 = mybir.dt.uint8
+FP8 = mybir.dt.float8_e4m3fn
+FP8X4 = mybir.dt.float8_e4m3fn_x4
+ACT = mybir.ActivationFunctionType
+ALU = mybir.AluOpType
+
+SCALE0 = 1.0 / math.sqrt(CIN)
+SCALE1 = 1.0 / math.sqrt(HID)
+
+
+def tile_cnn_pa_t_kernel(tc, x_bytes, x_scale, w0, w1, out):
+    nc = tc.nc
+
+    with ExitStack() as ctx:
+        keep = ctx.enter_context(tc.tile_pool(name="keep", bufs=1))
+        xin = ctx.enter_context(tc.tile_pool(name="xin", bufs=8))
+        outp = ctx.enter_context(tc.tile_pool(name="outp", bufs=4))
+        work = ctx.enter_context(tc.tile_pool(name="work", bufs=3))
+        psum = ctx.enter_context(tc.psum_pool(name="psum", bufs=4))
+        ctx.enter_context(tc.manual_schedule())
+
+        scale_rows = x_scale.rearrange("o (g p c) x -> g p (o c x)", g=G, p=P, c=2)
+        sc = []
+        for g in range(G):
+            sc_g = keep.tile([P, 2], F32, name="sc_%d" % g)
+            nc.scalar.dma_start(out=sc_g[:], in_=scale_rows[g])
+            sc.append(sc_g)
+        xv = x_bytes.rearrange("b (g p c) d -> b p g (c d)", g=G, p=P, c=2)
+        x_sb = []
+        for b in range(BS):
+            x_t = xin.tile([P, G, 2 * D], U8, name="x_t", align_bytes=64)
+            x_sb.append(x_t)
+        w0_sb = keep.tile([P, 2 * 2 * CIN], BF16, name="w0_sb", align_bytes=64)
+        w1_sb = keep.tile([P, 2 * 2 * HID], BF16, name="w1_sb", align_bytes=64)
+        for g, c in ((0, 1), (0, 0), (1, 1), (1, 0)):
+            nc.sync.dma_start(out=x_sb[0][:, g, c * D : (c + 1) * D], in_=xv[0][:, g, c * D : (c + 1) * D])
+        nc.sync.dma_start(out=x_sb[1][:, 0, :], in_=xv[1][:, 0, :])
+        nc.sync.dma_start(out=w0_sb[:], in_=w0.rearrange("(m t) c k -> m (t c k)", t=2))
+        nc.sync.dma_start(out=x_sb[1][:, 1, :], in_=xv[1][:, 1, :])
+        nc.sync.dma_start(out=w1_sb[:], in_=w1.rearrange("(m t) c k -> m (t c k)", t=2))
+        for b in range(2, BS):
+            nc.sync.dma_start(out=x_sb[b][:], in_=xv[b])
+
+        warm = keep.tile([P, 1], F32, name="warm")
+        nc.vector.memset(warm[:], 0.0)
+        nc.scalar.activation(out=warm[:], in_=warm[:], func=ACT.Relu)
+        ident = keep.tile([P, P], F32, name="ident")
+        make_identity(nc, ident[:])
+
+        w0_c = keep.tile([P, G * HID], U32, name="w0_c", align_bytes=64)
+        w0_s = keep.tile([P, G * HID], U8, name="w0_s", align_bytes=64)
+        w0_g = keep.tile([P, G * HID * 4], BF16, name="w0_g", align_bytes=64)
+        w1_c = keep.tile([P, OUT_DIM], U32, name="w1_c", align_bytes=64)
+        w1_s = keep.tile([P, OUT_DIM], U8, name="w1_s", align_bytes=64)
+        w1_g = keep.tile([P, OUT_DIM * 4], BF16, name="w1_g", align_bytes=64)
+
+        state = {}
+
+        def new(key, pool, shape, dtype, name):
+            if key not in state:
+                state[key] = pool.tile(shape, dtype, name=name, align_bytes=64)
+            return state[key]
+
+        def transpose_weights(w_sb, row, first, key):
+            words = w_sb[:].bitcast(F32)
+            bank = psum.tile([P, 2, 2, P], F32, name="bank2", tag="bank2")
+            for t in range(2):
+                for u in range(2):
+                    lo = row * t + first
+                    nc.tensor.transpose(bank[:, t, u, :], words[:, lo + u : lo + 256 : 2], ident[:])
+            state[key] = bank
+
+        def weights_out(engine_copy, key, dst):
+            engine_copy(
+                out=dst.bitcast(F32).rearrange("p (t m u) -> p t m u", t=2, u=2),
+                in_=state[key][:].rearrange("p t u m -> p t m u"),
+            )
+
+        def x_values(b, g, c, lo=0, n=Q):
+            return x_sb[b][:, g, c * D + 2 * lo : c * D + 2 * (lo + n)].bitcast(FP8)
+
+        def widen(engine, b, g, c):
+            tmp = new(("tmp", b), work, [P, G, 2, D], BF16, "tmp")
+            factor = sc[g][:, c : c + 1]
+            if engine == "S":
+                nc.scalar.activation(out=tmp[:, g, c, :], in_=x_values(b, g, c), func=ACT.Copy, scale=factor)
+            else:
+                nc.vector.tensor_scalar(out=tmp[:, g, c, :], in0=x_values(b, g, c), scalar1=factor, scalar2=None, op0=ALU.mult)
+
+        def interleave(b, g0=0, g1=G, lo=0, n=Q):
+            grp = new(("grp", b), work, [P, G * Q * 4], BF16, "grp")
+            words = state["tmp", b][:].rearrange("p g c d -> p (g c d)").bitcast(F32)
+            nc.vector.tensor_copy(
+                out=grp[:].bitcast(F32).rearrange("p (g q c) -> p g q c", g=G, c=2)[:, g0:g1, lo : lo + n, :],
+                in_=words.rearrange("p (g c q) -> p g q c", g=G, c=2)[:, g0:g1, lo : lo + n, :],
+            )
+
+        def quantize_x(b, lo=0, n=G * Q):
+            codes = new(("xc", b), work, [P, G * Q], U32, "xc")
+            scales = new(("xs", b), work, [P, G * Q], U8, "xs")
+            nc.vector.quantize_mx(
+                out=codes[:, lo : lo + n].bitcast(FP8X4),
+                scales=scales[:, lo : lo + n],
+                in_=state["grp", b][:, 4 * lo : 4 * (lo + n)],
+            )
+
+        def layer1(b, lo, n=HALF):
+            bank = psum.tile([P, 2, n], F32, name="bank1", tag="bank1")
+            for t in range(2):
+                for g in range(G):
+                    cols = slice(g * Q + lo, g * Q + lo + n)
+                    wcols = slice(g * HID + t * P, g * HID + (t + 1) * P)
+                    nc.tensor.matmul_mx(
+                        out=bank[:, t, :],
+                        lhsT=w0_c[:, wcols].bitcast(FP8X4),
+                        lhsT_scale=w0_s[:, wcols],
+                        rhs=state["xc", b][:, cols].bitcast(FP8X4),
+                        rhs_scale=state["xs", b][:, cols],
+                        start=(g == 0),
+                        stop=(g == G - 1),
+                    )
+            state["bank1", b, lo] = bank
+
+        def hidden(engine, b, lo, n=HALF):
+            h = new(("h", b), work, [P, R * 4], BF16, "hgrp")
+            dst = h[:, 2 * lo : 2 * (lo + n)].rearrange("p (r c k) -> p r c k", c=2, k=2)
+            z = state["bank1", b, lo][:].rearrange("p c (r k) -> p r c k", k=2)
+            if engine == "S":
+                nc.scalar.activation(out=dst, in_=z, func=ACT.Relu, scale=SCALE0)
+            else:
+                nc.vector.tensor_scalar(out=dst, in0=z, scalar1=SCALE0, scalar2=0.0, op0=ALU.mult, op1=ALU.max)
+
+        def quantize_h(b, lo=0, n=R):
+            codes = new(("hc", b), work, [P, R], U32, "hc")
+            scales = new(("hs", b), work, [P, R], U8, "hs")
+            nc.vector.quantize_mx(
+                out=codes[:, lo : lo + n].bitcast(FP8X4),
+                scales=scales[:, lo : lo + n],
+                in_=state["h", b][:, 4 * lo : 4 * (lo + n)],
+            )
+
+        def layer2(b, lo=0, n=R):
+            bank = psum.tile([P, 2, n], F32, name="bank2", tag="bank2")
+            for t in range(2):
+                wcols = slice(t * P, (t + 1) * P)
+                nc.tensor.matmul_mx(
+                    out=bank[:, t, :],
+                    lhsT=w1_c[:, wcols].bitcast(FP8X4),
+                    lhsT_scale=w1_s[:, wcols],
+                    rhs=state["hc", b][:, lo : lo + n].bitcast(FP8X4),
+                    rhs_scale=state["hs", b][:, lo : lo + n],
+                    start=True,
+                    stop=True,
+                )
+            state["bank2", b, lo] = bank
+
+        def finish(engine, b, lo=0, n=R):
+            o_sb = outp.tile([P, 2, n], F32, name="o_sb", tag="o_sb")
+            bank = state["bank2", b, lo]
+            if engine == "S":
+                nc.scalar.activation(out=o_sb[:], in_=bank[:], func=ACT.Relu, scale=SCALE1)
+            else:
+                nc.vector.tensor_scalar(out=o_sb[:], in0=bank[:], scalar1=SCALE1, scalar2=0.0, op0=ALU.mult, op1=ALU.max)
+            nc.sync.dma_start(out=out[b].rearrange("(m t) r -> m t r", t=2)[:, :, lo : lo + n], in_=o_sb[:])
+
+        def quantize_w(src, codes, scales):
+            nc.vector.quantize_mx(out=codes[:].bitcast(FP8X4), scales=scales[:], in_=src[:])
+
+        LAST = BS - 1
+        widen("S", 0, 0, 1)
+        widen("V", 0, 0, 0)
+        widen("S", 0, 1, 1)
+        widen("V", 0, 1, 0)
+        widen("S", 1, 0, 1)
+        transpose_weights(w0_sb, 512, 0, 0)
+        transpose_weights(w0_sb, 512, 256, 1)
+        transpose_weights(w1_sb, 256, 0, 2)
+        weights_out(nc.scalar.copy, 0, w0_g[:, 0 : HID * 4])
+        weights_out(nc.scalar.copy, 1, w0_g[:, HID * 4 :])
+        interleave(0, 0, 1)
+        widen("V", 1, 0, 0)
+        interleave(0, 1, 2)
+        quantize_x(0, 0, Q)
+        widen("S", 1, 1, 1)
+        quantize_x(0, Q, Q)
+        widen("V", 1, 1, 0)
+        quantize_w(w0_g, w0_c, w0_s)
+        layer1(0, 0)
+        layer1(0, HALF)
+        weights_out(nc.vector.tensor_copy, 2, w1_g[:])
+        interleave(1)
+        widen("S", 2, 0, 1)
+        widen("S", 2, 1, 1)
+        quantize_w(w1_g, w1_c, w1_s)
+        for i in range(2, LAST):
+            hidden("S", i - 2, 0)
+            hidden("S", i - 2, HALF)
+            widen("S", i + 1, 0, 1)
+            widen("S", i + 1, 1, 1)
+            if i + 1 == LAST:
+                widen("S", LAST, 1, 0)
+            widen("V", i, 0, 0)
+            widen("V", i, 1, 0)
+            quantize_x(i - 1)
+            layer1(i - 1, 0)
+            layer1(i - 1, HALF)
+            quantize_h(i - 2)
+            layer2(i - 2)
+            interleave(i)
+            if i >= 3:
+                finish("S", i - 3)
+        hidden("S", LAST - 2, 0)
+        hidden("S", LAST - 2, HALF)
+        widen("V", LAST, 0, 0)
+        quantize_x(LAST - 1)
+        layer1(LAST - 1, 0)
+        layer1(LAST - 1, HALF)
+        finish("S", LAST - 3)
+        interleave(LAST, 0, G, 0, HALF)
+        hidden("S", LAST - 1, 0)
+        hidden("S", LAST - 1, HALF)
+        interleave(LAST, 0, G, HALF, HALF)
+        quantize_h(LAST - 2)
+        layer2(LAST - 2)
+        quantize_x(LAST, 0, HALF)
+        quantize_x(LAST, Q, HALF)
+        layer1(LAST, 0)
+        quantize_x(LAST, HALF, HALF)
+        quantize_x(LAST, Q + HALF, HALF)
+        layer1(LAST, HALF, HALF // 2)
+        layer1(LAST, HALF + HALF // 2, HALF // 2)
+        finish("S", LAST - 2)
+        quantize_h(LAST - 1)
+        layer2(LAST - 1)
+        hidden("S", LAST, 0)
+        hidden("V", LAST, HALF, HALF // 2)
+        quantize_h(LAST, 0, R // 2)
+        layer2(LAST, 0, R // 2)
+        hidden("S", LAST, HALF + HALF // 2, HALF // 2)
+        finish("V", LAST - 1)
+        quantize_h(LAST, R // 2, R // 2)
+        layer2(LAST, R // 2, R // 2)
+        finish("S", LAST, 0, R // 2)
+        finish("V", LAST, R // 2, R // 2)

@@ -9,7 +9,7 @@ P = 128
 Q = D // 2
 R = Q // 2
 G = 2
-HALF = Q // 2
+BANK_N = 256
 
 FLOPS = 2 * BS * Q * HID * (2 * CIN) + 2 * BS * R * OUT_DIM * (2 * HID)
 
@@ -31,46 +31,10 @@ def tile_cnn_pa_t_kernel(tc, x_bytes, x_scale, w0, w1, out):
 
     with ExitStack() as ctx:
         keep = ctx.enter_context(tc.tile_pool(name="keep", bufs=1))
-        xin = ctx.enter_context(tc.tile_pool(name="xin", bufs=8))
-        outp = ctx.enter_context(tc.tile_pool(name="outp", bufs=4))
-        work = ctx.enter_context(tc.tile_pool(name="work", bufs=3))
-        psum = ctx.enter_context(tc.psum_pool(name="psum", bufs=4))
+        outp = ctx.enter_context(tc.tile_pool(name="outp", bufs=6))
+        work = ctx.enter_context(tc.tile_pool(name="work", bufs=4))
+        psum = ctx.enter_context(tc.psum_pool(name="psum", bufs=8))
         ctx.enter_context(tc.manual_schedule())
-
-        scale_rows = x_scale.rearrange("o (g p c) x -> g p (o c x)", g=G, p=P, c=2)
-        sc = []
-        for g in range(G):
-            sc_g = keep.tile([P, 2], F32, name="sc_%d" % g)
-            nc.scalar.dma_start(out=sc_g[:], in_=scale_rows[g])
-            sc.append(sc_g)
-        xv = x_bytes.rearrange("b (g p c) d -> b p g (c d)", g=G, p=P, c=2)
-        x_sb = []
-        for b in range(BS):
-            x_t = xin.tile([P, G, 2 * D], U8, name="x_t", align_bytes=64)
-            x_sb.append(x_t)
-        w0_sb = keep.tile([P, 2 * 2 * CIN], BF16, name="w0_sb", align_bytes=64)
-        w1_sb = keep.tile([P, 2 * 2 * HID], BF16, name="w1_sb", align_bytes=64)
-        for g, c in ((0, 1), (0, 0), (1, 1), (1, 0)):
-            nc.sync.dma_start(out=x_sb[0][:, g, c * D : (c + 1) * D], in_=xv[0][:, g, c * D : (c + 1) * D])
-        nc.sync.dma_start(out=x_sb[1][:, 0, :], in_=xv[1][:, 0, :])
-        nc.sync.dma_start(out=w0_sb[:], in_=w0.rearrange("(m t) c k -> m (t c k)", t=2))
-        nc.sync.dma_start(out=x_sb[1][:, 1, :], in_=xv[1][:, 1, :])
-        nc.sync.dma_start(out=w1_sb[:], in_=w1.rearrange("(m t) c k -> m (t c k)", t=2))
-        for b in range(2, BS):
-            nc.sync.dma_start(out=x_sb[b][:], in_=xv[b])
-
-        warm = keep.tile([P, 1], F32, name="warm")
-        nc.vector.memset(warm[:], 0.0)
-        nc.scalar.activation(out=warm[:], in_=warm[:], func=ACT.Relu)
-        ident = keep.tile([P, P], F32, name="ident")
-        make_identity(nc, ident[:])
-
-        w0_c = keep.tile([P, G * HID], U32, name="w0_c", align_bytes=64)
-        w0_s = keep.tile([P, G * HID], U8, name="w0_s", align_bytes=64)
-        w0_g = keep.tile([P, G * HID * 4], BF16, name="w0_g", align_bytes=64)
-        w1_c = keep.tile([P, OUT_DIM], U32, name="w1_c", align_bytes=64)
-        w1_s = keep.tile([P, OUT_DIM], U8, name="w1_s", align_bytes=64)
-        w1_g = keep.tile([P, OUT_DIM * 4], BF16, name="w1_g", align_bytes=64)
 
         state = {}
 
@@ -79,9 +43,35 @@ def tile_cnn_pa_t_kernel(tc, x_bytes, x_scale, w0, w1, out):
                 state[key] = pool.tile(shape, dtype, name=name, align_bytes=64)
             return state[key]
 
+        sc = keep.tile([P, G, 8], F32, name="sc")
+        nc.scalar.dma_start(out=sc[:, :, 0:2], in_=x_scale.rearrange("o (g p c) x -> p g (o c x)", g=G, p=P, c=2))
+        xv = x_bytes.rearrange("b (g p c) d -> b p g c d", g=G, p=P, c=2)
+
+        def load_x(u, g0=0, g1=G):
+            b, lo, n = u
+            x_t = new(("x", u), keep, [P, G, 2, 2 * n], U8, "x_%d_%d" % (b, lo))
+            if n == Q:
+                nc.sync.dma_start(out=x_t[:, g0:g1], in_=xv[b][:, g0:g1])
+            else:
+                for g in range(g0, g1):
+                    nc.sync.dma_start(out=x_t[:, g], in_=xv[b][:, g, :, 2 * lo : 2 * (lo + n)])
+
+        w0_sb = keep.tile([P, 2 * 2 * CIN], BF16, name="w0_sb", align_bytes=64)
+        w1_sb = keep.tile([P, 2 * 2 * HID], BF16, name="w1_sb", align_bytes=64)
+
+        def load_w(w_sb, w):
+            nc.sync.dma_start(out=w_sb[:], in_=w.rearrange("(m t) c k -> m (t c k)", t=2))
+
+        w0_c = keep.tile([P, G * HID], U32, name="w0_c", align_bytes=64)
+        w0_s = keep.tile([P, G * HID], U8, name="w0_s", align_bytes=64)
+        w0_g = keep.tile([P, G * HID * 4], BF16, name="w0_g", align_bytes=64)
+        w1_c = keep.tile([P, OUT_DIM], U32, name="w1_c", align_bytes=64)
+        w1_s = keep.tile([P, OUT_DIM], U8, name="w1_s", align_bytes=64)
+        w1_g = keep.tile([P, OUT_DIM * 4], BF16, name="w1_g", align_bytes=64)
+
         def transpose_weights(w_sb, row, first, key):
             words = w_sb[:].bitcast(F32)
-            bank = psum.tile([P, 2, 2, P], F32, name="bank2", tag="bank2")
+            bank = psum.tile([P, 2, 2, P], F32, name="bank2", tag="bank")
             for t in range(2):
                 for u in range(2):
                     lo = row * t + first
@@ -94,52 +84,100 @@ def tile_cnn_pa_t_kernel(tc, x_bytes, x_scale, w0, w1, out):
                 in_=state[key][:].rearrange("p t u m -> p t m u"),
             )
 
-        def x_values(b, g, c, lo=0, n=Q):
-            return x_sb[b][:, g, c * D + 2 * lo : c * D + 2 * (lo + n)].bitcast(FP8)
+        def quantize_w(src, codes, scales):
+            nc.vector.quantize_mx(out=codes[:].bitcast(FP8X4), scales=scales[:], in_=src[:])
 
-        def widen(engine, b, g, c):
-            tmp = new(("tmp", b), work, [P, G, 2, D], BF16, "tmp")
-            factor = sc[g][:, c : c + 1]
+        def widen(engine, u, g, c, first=0, last=None):
+            b, lo, n = u
+            last = last or 2 * n
+            values = state["x", u][:, g, c, first:last].bitcast(FP8)
+            tmp = new(("tmp", u), work, [P, G * 2 * 2 * n], BF16, "tmp")
+            row = (2 * g + c) * 2 * n
+            dst = tmp[:, row + first : row + last]
+            factor = sc[:, g, c : c + 1]
             if engine == "S":
-                nc.scalar.activation(out=tmp[:, g, c, :], in_=x_values(b, g, c), func=ACT.Copy, scale=factor)
+                nc.scalar.activation(out=dst, in_=values, func=ACT.Copy, scale=factor)
             else:
-                nc.vector.tensor_scalar(out=tmp[:, g, c, :], in0=x_values(b, g, c), scalar1=factor, scalar2=None, op0=ALU.mult)
+                nc.vector.tensor_scalar(out=dst, in0=values, scalar1=factor, scalar2=None, op0=ALU.mult)
 
-        def interleave(b, g0=0, g1=G, lo=0, n=Q):
-            grp = new(("grp", b), work, [P, G * Q * 4], BF16, "grp")
-            words = state["tmp", b][:].rearrange("p g c d -> p (g c d)").bitcast(F32)
+        def interleave(u, g0=0, g1=G, src=None):
+            b, lo, n = u
+            src = src or u
+            first = lo - src[1]
+            grp = new(("grp", u), work, [P, G * n * 4], BF16, "grp")
+            words = state["tmp", src][:].bitcast(F32).rearrange("p (g c q) -> p g q c", g=G, c=2)
             nc.vector.tensor_copy(
-                out=grp[:].bitcast(F32).rearrange("p (g q c) -> p g q c", g=G, c=2)[:, g0:g1, lo : lo + n, :],
-                in_=words.rearrange("p (g c q) -> p g q c", g=G, c=2)[:, g0:g1, lo : lo + n, :],
+                out=grp[:].bitcast(F32).rearrange("p (g q c) -> p g q c", g=G, c=2)[:, g0:g1],
+                in_=words[:, g0:g1, first : first + n, :],
             )
 
-        def quantize_x(b, lo=0, n=G * Q):
-            codes = new(("xc", b), work, [P, G * Q], U32, "xc")
-            scales = new(("xs", b), work, [P, G * Q], U8, "xs")
+        def quantize_x(u, g0=0, g1=G):
+            b, lo, n = u
+            codes = new(("xc", u), work, [P, G * n], U32, "xc")
+            scales = new(("xs", u), work, [P, G * n], U8, "xs")
             nc.vector.quantize_mx(
-                out=codes[:, lo : lo + n].bitcast(FP8X4),
-                scales=scales[:, lo : lo + n],
-                in_=state["grp", b][:, 4 * lo : 4 * (lo + n)],
+                out=codes[:, g0 * n : g1 * n].bitcast(FP8X4),
+                scales=scales[:, g0 * n : g1 * n],
+                in_=state["grp", u][:, 4 * g0 * n : 4 * g1 * n],
             )
 
-        def layer1(b, lo, n=HALF):
-            bank = psum.tile([P, 2, n], F32, name="bank1", tag="bank1")
-            for t in range(2):
-                for g in range(G):
-                    cols = slice(g * Q + lo, g * Q + lo + n)
-                    wcols = slice(g * HID + t * P, g * HID + (t + 1) * P)
-                    nc.tensor.matmul_mx(
-                        out=bank[:, t, :],
-                        lhsT=w0_c[:, wcols].bitcast(FP8X4),
-                        lhsT_scale=w0_s[:, wcols],
-                        rhs=state["xc", b][:, cols].bitcast(FP8X4),
-                        rhs_scale=state["xs", b][:, cols],
-                        start=(g == 0),
-                        stop=(g == G - 1),
-                    )
-            state["bank1", b, lo] = bank
+        def layer1(u):
+            b, lo, n = u
+            for first in range(0, n, BANK_N):
+                m = min(n, BANK_N)
+                bank = psum.tile([P, 2, m], F32, name="bank1", tag="bank")
+                for t in range(2):
+                    for g in range(G):
+                        cols = slice(g * n + first, g * n + first + m)
+                        wcols = slice(g * HID + t * P, g * HID + (t + 1) * P)
+                        nc.tensor.matmul_mx(
+                            out=bank[:, t, :],
+                            lhsT=w0_c[:, wcols].bitcast(FP8X4),
+                            lhsT_scale=w0_s[:, wcols],
+                            rhs=state["xc", u][:, cols].bitcast(FP8X4),
+                            rhs_scale=state["xs", u][:, cols],
+                            start=(g == 0),
+                            stop=(g == G - 1),
+                        )
+                state["bank1", b, lo + first] = bank
 
-        def hidden(engine, b, lo, n=HALF):
+        def layer1_pass(u, g):
+            b, lo, n = u
+            if g == 0:
+                state["bank1", b, lo] = psum.tile([P, 2, n], F32, name="bank1", tag="bank")
+            for t in range(2):
+                cols = slice(g * n, (g + 1) * n)
+                wcols = slice(g * HID + t * P, g * HID + (t + 1) * P)
+                nc.tensor.matmul_mx(
+                    out=state["bank1", b, lo][:, t, :],
+                    lhsT=w0_c[:, wcols].bitcast(FP8X4),
+                    lhsT_scale=w0_s[:, wcols],
+                    rhs=state["xc", u][:, cols].bitcast(FP8X4),
+                    rhs_scale=state["xs", u][:, cols],
+                    start=(g == 0 and t == 0),
+                    stop=(g == G - 1 and t == 1),
+                )
+
+        def layer2_tile(engine, b, lo, n, t):
+            bank = psum.tile([P, n], F32, name="bank3", tag="bank")
+            wcols = slice(t * P, (t + 1) * P)
+            nc.tensor.matmul_mx(
+                out=bank[:],
+                lhsT=w1_c[:, wcols].bitcast(FP8X4),
+                lhsT_scale=w1_s[:, wcols],
+                rhs=state["hc", b][:, lo : lo + n].bitcast(FP8X4),
+                rhs_scale=state["hs", b][:, lo : lo + n],
+                start=True,
+                stop=True,
+            )
+            o_sb = outp.tile([P, n], F32, name="o_sb", tag="o_sb")
+            if engine == "S":
+                nc.scalar.activation(out=o_sb[:], in_=bank[:], func=ACT.Relu, scale=SCALE1)
+            else:
+                nc.vector.tensor_scalar(out=o_sb[:], in0=bank[:], scalar1=SCALE1, scalar2=0.0, op0=ALU.mult, op1=ALU.max)
+            nc.sync.dma_start(out=out[b].rearrange("(m t) r -> m t r", t=2)[:, t, lo : lo + n], in_=o_sb[:])
+
+        def hidden(engine, b, lo, n=BANK_N):
             h = new(("h", b), work, [P, R * 4], BF16, "hgrp")
             dst = h[:, 2 * lo : 2 * (lo + n)].rearrange("p (r c k) -> p r c k", c=2, k=2)
             z = state["bank1", b, lo][:].rearrange("p c (r k) -> p r c k", k=2)
@@ -158,7 +196,7 @@ def tile_cnn_pa_t_kernel(tc, x_bytes, x_scale, w0, w1, out):
             )
 
         def layer2(b, lo=0, n=R):
-            bank = psum.tile([P, 2, n], F32, name="bank2", tag="bank2")
+            bank = psum.tile([P, 2, n], F32, name="bank2", tag="bank")
             for t in range(2):
                 wcols = slice(t * P, (t + 1) * P)
                 nc.tensor.matmul_mx(
@@ -181,82 +219,101 @@ def tile_cnn_pa_t_kernel(tc, x_bytes, x_scale, w0, w1, out):
                 nc.vector.tensor_scalar(out=o_sb[:], in0=bank[:], scalar1=SCALE1, scalar2=0.0, op0=ALU.mult, op1=ALU.max)
             nc.sync.dma_start(out=out[b].rearrange("(m t) r -> m t r", t=2)[:, :, lo : lo + n], in_=o_sb[:])
 
-        def quantize_w(src, codes, scales):
-            nc.vector.quantize_mx(out=codes[:].bitcast(FP8X4), scales=scales[:], in_=src[:])
-
         LAST = BS - 1
-        widen("S", 0, 0, 1)
-        widen("V", 0, 0, 0)
-        widen("S", 0, 1, 1)
-        widen("V", 0, 1, 0)
-        widen("S", 1, 0, 1)
+        full = [(b, 0, Q) for b in range(BS)]
+        a0, b0 = (0, 0, Q // 2), (0, Q // 2, Q // 2)
+        a7, b7, c7 = (LAST, 0, Q // 2), (LAST, Q // 2, Q // 4), (LAST, 3 * Q // 4, Q // 4)
+        load_x(a0)
+        load_x(b0)
+        load_x(full[1], 0, 1)
+        load_x(full[1], 1, 2)
+        load_x(full[2], 0, 1)
+        load_w(w0_sb, w0)
+        load_x(full[2], 1, 2)
+        load_w(w1_sb, w1)
+        for b in range(3, BS):
+            load_x(full[b])
+
+        warm = keep.tile([P, 1], F32, name="warm")
+        nc.vector.memset(warm[:], 0.0)
+        nc.scalar.activation(out=warm[:], in_=warm[:], func=ACT.Relu)
+        ident = keep.tile([P, P], F32, name="ident")
+        make_identity(nc, ident[:])
+
+        widen("V", a0, 0, 0)
+        widen("S", a0, 0, 1)
+        widen("V", a0, 1, 0)
+        widen("S", a0, 1, 1)
+        widen("V", b0, 0, 0)
+        widen("S", b0, 0, 1)
+        widen("V", b0, 1, 0)
+        widen("V", b0, 1, 1)
+        widen("S", full[1], 0, 1)
+        widen("S", full[1], 1, 1)
+        interleave(a0)
+        widen("V", full[1], 0, 0)
+        quantize_x(a0)
+        interleave(b0)
+        widen("V", full[1], 1, 0)
+        quantize_x(b0)
         transpose_weights(w0_sb, 512, 0, 0)
         transpose_weights(w0_sb, 512, 256, 1)
         transpose_weights(w1_sb, 256, 0, 2)
+        widen("S", full[2], 0, 1)
         weights_out(nc.scalar.copy, 0, w0_g[:, 0 : HID * 4])
         weights_out(nc.scalar.copy, 1, w0_g[:, HID * 4 :])
-        interleave(0, 0, 1)
-        widen("V", 1, 0, 0)
-        interleave(0, 1, 2)
-        quantize_x(0, 0, Q)
-        widen("S", 1, 1, 1)
-        quantize_x(0, Q, Q)
-        widen("V", 1, 1, 0)
+        widen("S", full[2], 1, 1)
+        interleave(full[1])
+        widen("V", full[2], 0, 0)
+        widen("V", full[2], 1, 0)
         quantize_w(w0_g, w0_c, w0_s)
-        layer1(0, 0)
-        layer1(0, HALF)
-        weights_out(nc.vector.tensor_copy, 2, w1_g[:])
-        interleave(1)
-        widen("S", 2, 0, 1)
-        widen("S", 2, 1, 1)
+        layer1(a0)
+        layer1(b0)
+        quantize_x(full[1])
+        layer1(full[1])
+        weights_out(nc.scalar.copy, 2, w1_g[:])
+        widen("S", full[3], 0, 1)
+        hidden("S", 0, 0)
+        hidden("S", 0, BANK_N)
         quantize_w(w1_g, w1_c, w1_s)
         for i in range(2, LAST):
-            hidden("S", i - 2, 0)
-            hidden("S", i - 2, HALF)
-            widen("S", i + 1, 0, 1)
-            widen("S", i + 1, 1, 1)
-            if i + 1 == LAST:
-                widen("S", LAST, 1, 0)
-            widen("V", i, 0, 0)
-            widen("V", i, 1, 0)
-            quantize_x(i - 1)
-            layer1(i - 1, 0)
-            layer1(i - 1, HALF)
+            widen("S", full[i + 1], 1, 1)
+            hidden("S", i - 1, 0)
+            hidden("S", i - 1, BANK_N)
+            interleave(full[i])
             quantize_h(i - 2)
             layer2(i - 2)
-            interleave(i)
-            if i >= 3:
-                finish("S", i - 3)
-        hidden("S", LAST - 2, 0)
-        hidden("S", LAST - 2, HALF)
-        widen("V", LAST, 0, 0)
-        quantize_x(LAST - 1)
-        layer1(LAST - 1, 0)
-        layer1(LAST - 1, HALF)
+            widen("V", full[i + 1], 0, 0)
+            widen("V", full[i + 1], 1, 0)
+            quantize_x(full[i])
+            layer1(full[i])
+            if i < LAST - 1:
+                finish("S", i - 2)
+                widen("S", full[i + 2], 0, 1)
+        interleave(a7, src=full[LAST])
+        interleave(b7, src=full[LAST])
         finish("S", LAST - 3)
-        interleave(LAST, 0, G, 0, HALF)
         hidden("S", LAST - 1, 0)
-        hidden("S", LAST - 1, HALF)
-        interleave(LAST, 0, G, HALF, HALF)
+        hidden("S", LAST - 1, BANK_N)
+        quantize_x(a7)
+        layer1(a7)
         quantize_h(LAST - 2)
         layer2(LAST - 2)
-        quantize_x(LAST, 0, HALF)
-        quantize_x(LAST, Q, HALF)
-        layer1(LAST, 0)
-        quantize_x(LAST, HALF, HALF)
-        quantize_x(LAST, Q + HALF, HALF)
-        layer1(LAST, HALF, HALF // 2)
-        layer1(LAST, HALF + HALF // 2, HALF // 2)
-        finish("S", LAST - 2)
+        interleave(c7, src=full[LAST])
+        quantize_x(b7)
+        layer1(b7)
+        quantize_x(c7)
+        layer1(c7)
         quantize_h(LAST - 1)
         layer2(LAST - 1)
+        finish("V", LAST - 2)
         hidden("S", LAST, 0)
-        hidden("V", LAST, HALF, HALF // 2)
+        hidden("S", LAST, b7[1], b7[2])
+        hidden("S", LAST, c7[1], c7[2])
         quantize_h(LAST, 0, R // 2)
         layer2(LAST, 0, R // 2)
-        hidden("S", LAST, HALF + HALF // 2, HALF // 2)
-        finish("V", LAST - 1)
         quantize_h(LAST, R // 2, R // 2)
         layer2(LAST, R // 2, R // 2)
-        finish("S", LAST, 0, R // 2)
-        finish("V", LAST, R // 2, R // 2)
+        finish("S", LAST - 1)
+        finish("V", LAST, 0, R // 2)
+        finish("S", LAST, R // 2, R // 2)

@@ -32,7 +32,7 @@ def tile_cnn_pa_t_kernel(tc, x_bytes, x_scale, w0, w1, out):
     with ExitStack() as ctx:
         keep = ctx.enter_context(tc.tile_pool(name="keep", bufs=1))
         outp = ctx.enter_context(tc.tile_pool(name="outp", bufs=6))
-        work = ctx.enter_context(tc.tile_pool(name="work", bufs=4))
+        work = ctx.enter_context(tc.tile_pool(name="work", bufs=5))
         psum = ctx.enter_context(tc.psum_pool(name="psum", bufs=8))
         ctx.enter_context(tc.manual_schedule())
 
@@ -56,11 +56,10 @@ def tile_cnn_pa_t_kernel(tc, x_bytes, x_scale, w0, w1, out):
                 for g in range(g0, g1):
                     nc.sync.dma_start(out=x_t[:, g], in_=xv[b][:, g, :, 2 * lo : 2 * (lo + n)])
 
-        w0_sb = keep.tile([P, 2 * 2 * CIN], BF16, name="w0_sb", align_bytes=64)
-        w1_sb = keep.tile([P, 2 * 2 * HID], BF16, name="w1_sb", align_bytes=64)
-
-        def load_w(w_sb, w):
-            nc.sync.dma_start(out=w_sb[:], in_=w.rearrange("(m t) c k -> m (t c k)", t=2))
+        def load_w(key, w, g):
+            w_sb = new(("w", key), keep, [P, 2 * 512], BF16, "w_sb_%d" % key)
+            rows = w.rearrange("(m t) c k -> m t (c k)", t=2)[:, :, 512 * g : 512 * (g + 1)]
+            nc.sync.dma_start(out=w_sb[:].rearrange("p (t j) -> p t j", t=2), in_=rows)
 
         w0_c = keep.tile([P, G * HID], U32, name="w0_c", align_bytes=64)
         w0_s = keep.tile([P, G * HID], U8, name="w0_s", align_bytes=64)
@@ -69,12 +68,12 @@ def tile_cnn_pa_t_kernel(tc, x_bytes, x_scale, w0, w1, out):
         w1_s = keep.tile([P, OUT_DIM], U8, name="w1_s", align_bytes=64)
         w1_g = keep.tile([P, OUT_DIM * 4], BF16, name="w1_g", align_bytes=64)
 
-        def transpose_weights(w_sb, row, first, key):
-            words = w_sb[:].bitcast(F32)
+        def transpose_weights(key):
+            words = state["w", key][:].bitcast(F32)
             bank = psum.tile([P, 2, 2, P], F32, name="bank2", tag="bank")
             for t in range(2):
                 for u in range(2):
-                    lo = row * t + first
+                    lo = 256 * t
                     nc.tensor.transpose(bank[:, t, u, :], words[:, lo + u : lo + 256 : 2], ident[:])
             state[key] = bank
 
@@ -100,15 +99,18 @@ def tile_cnn_pa_t_kernel(tc, x_bytes, x_scale, w0, w1, out):
             else:
                 nc.vector.tensor_scalar(out=dst, in0=values, scalar1=factor, scalar2=None, op0=ALU.mult)
 
-        def interleave(u, g0=0, g1=G, src=None):
-            b, lo, n = u
-            src = src or u
+        def interleave(b, pieces):
+            lo, n = pieces[0][1], pieces[0][2]
+            src = pieces[0] if ("tmp", pieces[0]) in state else (b, 0, Q)
             first = lo - src[1]
-            grp = new(("grp", u), work, [P, G * n * 4], BF16, "grp")
-            words = state["tmp", src][:].bitcast(F32).rearrange("p (g c q) -> p g q c", g=G, c=2)
+            grp = work.tile([P, len(pieces) * G * n * 4], BF16, name="grp", align_bytes=64)
+            for j, u in enumerate(pieces):
+                state["grp", u] = grp[:, j * G * n * 4 : (j + 1) * G * n * 4]
+            words = state["tmp", src][:].bitcast(F32).rearrange("p (g c q) -> p g c q", g=G, c=2)
+            words = words[:, :, :, first : first + len(pieces) * n]
             nc.vector.tensor_copy(
-                out=grp[:].bitcast(F32).rearrange("p (g q c) -> p g q c", g=G, c=2)[:, g0:g1],
-                in_=words[:, g0:g1, first : first + n, :],
+                out=grp[:].bitcast(F32).rearrange("p (h g q c) -> p h g q c", g=G, q=n, c=2),
+                in_=words.rearrange("p g c (h q) -> p h g q c", q=n),
             )
 
         def quantize_x(u, g0=0, g1=G):
@@ -123,23 +125,21 @@ def tile_cnn_pa_t_kernel(tc, x_bytes, x_scale, w0, w1, out):
 
         def layer1(u):
             b, lo, n = u
-            for first in range(0, n, BANK_N):
-                m = min(n, BANK_N)
-                bank = psum.tile([P, 2, m], F32, name="bank1", tag="bank")
-                for t in range(2):
-                    for g in range(G):
-                        cols = slice(g * n + first, g * n + first + m)
-                        wcols = slice(g * HID + t * P, g * HID + (t + 1) * P)
-                        nc.tensor.matmul_mx(
-                            out=bank[:, t, :],
-                            lhsT=w0_c[:, wcols].bitcast(FP8X4),
-                            lhsT_scale=w0_s[:, wcols],
-                            rhs=state["xc", u][:, cols].bitcast(FP8X4),
-                            rhs_scale=state["xs", u][:, cols],
-                            start=(g == 0),
-                            stop=(g == G - 1),
-                        )
-                state["bank1", b, lo + first] = bank
+            bank = psum.tile([P, 2, n], F32, name="bank1", tag="bank")
+            for t in range(2):
+                for g in range(G):
+                    cols = slice(g * n, (g + 1) * n)
+                    wcols = slice(g * HID + t * P, g * HID + (t + 1) * P)
+                    nc.tensor.matmul_mx(
+                        out=bank[:, t, :],
+                        lhsT=w0_c[:, wcols].bitcast(FP8X4),
+                        lhsT_scale=w0_s[:, wcols],
+                        rhs=state["xc", u][:, cols].bitcast(FP8X4),
+                        rhs_scale=state["xs", u][:, cols],
+                        start=(g == 0),
+                        stop=(g == G - 1),
+                    )
+            state["bank1", b, lo] = bank
 
         def layer1_pass(u, g):
             b, lo, n = u
@@ -220,17 +220,22 @@ def tile_cnn_pa_t_kernel(tc, x_bytes, x_scale, w0, w1, out):
             nc.sync.dma_start(out=out[b].rearrange("(m t) r -> m t r", t=2)[:, :, lo : lo + n], in_=o_sb[:])
 
         LAST = BS - 1
+        EXTRA = 4
+        SHARE = 512
         full = [(b, 0, Q) for b in range(BS)]
-        a0, b0 = (0, 0, Q // 2), (0, Q // 2, Q // 2)
-        a7, b7, c7 = (LAST, 0, Q // 2), (LAST, Q // 2, Q // 4), (LAST, 3 * Q // 4, Q // 4)
+        lower = [(b, 0, Q // 2) for b in range(BS)]
+        upper = [(b, Q // 2, Q // 2) for b in range(BS)]
+        a0, b0 = lower[0], upper[0]
+        a7, b7, c7 = lower[LAST], (LAST, Q // 2, Q // 4), (LAST, 3 * Q // 4, Q // 4)
         load_x(a0)
         load_x(b0)
         load_x(full[1], 0, 1)
+        load_w(0, w0, 0)
         load_x(full[1], 1, 2)
+        load_w(1, w0, 1)
         load_x(full[2], 0, 1)
-        load_w(w0_sb, w0)
         load_x(full[2], 1, 2)
-        load_w(w1_sb, w1)
+        load_w(2, w1, 0)
         for b in range(3, BS):
             load_x(full[b])
 
@@ -239,6 +244,8 @@ def tile_cnn_pa_t_kernel(tc, x_bytes, x_scale, w0, w1, out):
         nc.scalar.activation(out=warm[:], in_=warm[:], func=ACT.Relu)
         ident = keep.tile([P, P], F32, name="ident")
         make_identity(nc, ident[:])
+        for key in range(3):
+            transpose_weights(key)
 
         widen("V", a0, 0, 0)
         widen("S", a0, 0, 1)
@@ -250,70 +257,87 @@ def tile_cnn_pa_t_kernel(tc, x_bytes, x_scale, w0, w1, out):
         widen("V", b0, 1, 1)
         widen("S", full[1], 0, 1)
         widen("S", full[1], 1, 1)
-        interleave(a0)
-        widen("V", full[1], 0, 0)
-        quantize_x(a0)
-        interleave(b0)
-        widen("V", full[1], 1, 0)
-        quantize_x(b0)
-        transpose_weights(w0_sb, 512, 0, 0)
-        transpose_weights(w0_sb, 512, 256, 1)
-        transpose_weights(w1_sb, 256, 0, 2)
         widen("S", full[2], 0, 1)
         weights_out(nc.scalar.copy, 0, w0_g[:, 0 : HID * 4])
         weights_out(nc.scalar.copy, 1, w0_g[:, HID * 4 :])
         widen("S", full[2], 1, 1)
-        interleave(full[1])
+        widen("S", full[3], 0, 1)
+        weights_out(nc.scalar.copy, 2, w1_g[:])
+        interleave(0, [a0])
+        widen("V", full[1], 0, 0)
+        quantize_x(a0)
+        interleave(0, [b0])
+        widen("V", full[1], 1, 0)
+        quantize_x(b0)
+        interleave(1, [lower[1], upper[1]])
         widen("V", full[2], 0, 0)
         widen("V", full[2], 1, 0)
         quantize_w(w0_g, w0_c, w0_s)
         layer1(a0)
         layer1(b0)
-        quantize_x(full[1])
-        layer1(full[1])
-        weights_out(nc.scalar.copy, 2, w1_g[:])
-        widen("S", full[3], 0, 1)
-        hidden("S", 0, 0)
-        hidden("S", 0, BANK_N)
-        quantize_w(w1_g, w1_c, w1_s)
+        quantize_x(lower[1])
+        layer1(lower[1])
         for i in range(2, LAST):
-            widen("S", full[i + 1], 1, 1)
-            hidden("S", i - 1, 0)
-            hidden("S", i - 1, BANK_N)
-            interleave(full[i])
-            quantize_h(i - 2)
-            layer2(i - 2)
-            widen("V", full[i + 1], 0, 0)
-            widen("V", full[i + 1], 1, 0)
-            quantize_x(full[i])
-            layer1(full[i])
+            late = i >= LAST - 2
             if i < LAST - 1:
-                finish("S", i - 2)
+                widen("S", full[i + 1], 1, 1)
+                if i + 1 == EXTRA:
+                    widen("S", full[i + 1], 1, 0, 0, SHARE)
+                hidden("S", i - 2, 0)
+                hidden("S", i - 2, BANK_N)
+            if not late:
                 widen("S", full[i + 2], 0, 1)
-        interleave(a7, src=full[LAST])
-        interleave(b7, src=full[LAST])
-        finish("S", LAST - 3)
-        hidden("S", LAST - 1, 0)
-        hidden("S", LAST - 1, BANK_N)
+            interleave(i, [lower[i], upper[i]])
+            quantize_x(upper[i - 1])
+            layer1(upper[i - 1])
+            widen("V", full[i + 1], 0, 0)
+            if i == 2:
+                quantize_w(w1_g, w1_c, w1_s)
+            elif i < LAST - 1:
+                quantize_h(i - 3)
+                layer2(i - 3)
+                if late:
+                    hidden("S", i - 1, 0)
+                    hidden("S", i - 1, BANK_N)
+                    widen("S", full[LAST], 0, 1)
+                    widen("S", full[LAST], 1, 1)
+                finish("S", i - 3)
+            else:
+                quantize_h(i - 3)
+                layer2(i - 3)
+                quantize_h(i - 2)
+                layer2(i - 2)
+                hidden("S", i - 1, 0)
+                hidden("S", i - 1, BANK_N)
+                finish("S", i - 3)
+            widen("V", full[i + 1], 1, 0, SHARE if i + 1 == EXTRA else 0)
+            quantize_x(lower[i])
+            layer1(lower[i])
+        interleave(LAST, [a7])
+        quantize_x(upper[LAST - 1])
+        layer1(upper[LAST - 1])
         quantize_x(a7)
         layer1(a7)
+        hidden("S", LAST - 1, 0)
+        finish("S", LAST - 3)
+        hidden("S", LAST - 1, BANK_N)
+        hidden("S", LAST, 0)
+        interleave(LAST, [b7, c7])
         quantize_h(LAST - 2)
         layer2(LAST - 2)
-        interleave(c7, src=full[LAST])
         quantize_x(b7)
         layer1(b7)
         quantize_x(c7)
         layer1(c7)
         quantize_h(LAST - 1)
         layer2(LAST - 1)
-        finish("V", LAST - 2)
-        hidden("S", LAST, 0)
-        hidden("S", LAST, b7[1], b7[2])
-        hidden("S", LAST, c7[1], c7[2])
         quantize_h(LAST, 0, R // 2)
         layer2(LAST, 0, R // 2)
+        finish("S", LAST - 2)
+        hidden("V", LAST, b7[1], b7[2])
+        hidden("S", LAST, c7[1], c7[2])
         quantize_h(LAST, R // 2, R // 2)
-        layer2(LAST, R // 2, R // 2)
         finish("S", LAST - 1)
         finish("V", LAST, 0, R // 2)
-        finish("S", LAST, R // 2, R // 2)
+        layer2_tile("V", LAST, R // 2, R // 2, 0)
+        layer2_tile("S", LAST, R // 2, R // 2, 1)

@@ -32,6 +32,7 @@ def tile_cnn_pa_t_kernel(tc, x_bytes, x_scale, w0, w1, out):
     with ExitStack() as ctx:
         keep = ctx.enter_context(tc.tile_pool(name="keep", bufs=1))
         outp = ctx.enter_context(tc.tile_pool(name="outp", bufs=6))
+        wide = ctx.enter_context(tc.tile_pool(name="wide", bufs=5))
         work = ctx.enter_context(tc.tile_pool(name="work", bufs=5))
         psum = ctx.enter_context(tc.psum_pool(name="psum", bufs=8))
         ctx.enter_context(tc.manual_schedule())
@@ -45,21 +46,28 @@ def tile_cnn_pa_t_kernel(tc, x_bytes, x_scale, w0, w1, out):
 
         sc = keep.tile([P, G, 8], F32, name="sc")
         nc.scalar.dma_start(out=sc[:, :, 0:2], in_=x_scale.rearrange("o (g p c) x -> p g (o c x)", g=G, p=P, c=2))
-        xv = x_bytes.rearrange("b (g p c) d -> b p g c d", g=G, p=P, c=2)
+        xv = x_bytes.rearrange("b (g p c) d -> p g c b d", g=G, p=P, c=2)
 
-        def load_x(u, g0=0, g1=G):
-            b, lo, n = u
-            x_t = new(("x", u), keep, [P, G, 2, 2 * n], U8, "x_%d_%d" % (b, lo))
-            if n == Q:
-                nc.sync.dma_start(out=x_t[:, g0:g1], in_=xv[b][:, g0:g1])
+        def load_x(span, g, c0=0, c1=2):
+            first, n = span
+            x_t = new(("x", span), keep, [P, G, 2, 2 * n], U8, "x_%d" % first)
+            b, lo = divmod(first, Q)
+            if n <= Q:
+                nc.sync.dma_start(out=x_t[:, g, c0:c1], in_=xv[:, g, c0:c1, b, 2 * lo : 2 * (lo + n)])
             else:
-                for g in range(g0, g1):
-                    nc.sync.dma_start(out=x_t[:, g], in_=xv[b][:, g, :, 2 * lo : 2 * (lo + n)])
+                for c in range(c0, c1):
+                    rows = x_t[:, g, c].rearrange("p (b d) -> p b d", d=D)
+                    nc.sync.dma_start(out=rows, in_=xv[:, g, c, b : b + n // Q])
 
-        def load_w(key, w, g):
-            w_sb = new(("w", key), keep, [P, 2 * 512], BF16, "w_sb_%d" % key)
-            rows = w.rearrange("(m t) c k -> m t (c k)", t=2)[:, :, 512 * g : 512 * (g + 1)]
-            nc.sync.dma_start(out=w_sb[:].rearrange("p (t j) -> p t j", t=2), in_=rows)
+        def load_batch(span):
+            x_t = new(("x", span), keep, [P, G, 2, D], U8, "x_%d" % span[0])
+            nc.sync.dma_start(out=x_t[:], in_=xv[:, :, :, span[0] // Q])
+
+        w0_sb = keep.tile([P, 2 * 2 * CIN], BF16, name="w0_sb", align_bytes=64)
+        w1_sb = keep.tile([P, 2 * 2 * HID], BF16, name="w1_sb", align_bytes=64)
+
+        def load_w(w_sb, w):
+            nc.sync.dma_start(out=w_sb[:], in_=w.rearrange("(m t) c k -> m (t c k)", t=2))
 
         w0_c = keep.tile([P, G * HID], U32, name="w0_c", align_bytes=64)
         w0_s = keep.tile([P, G * HID], U8, name="w0_s", align_bytes=64)
@@ -68,29 +76,29 @@ def tile_cnn_pa_t_kernel(tc, x_bytes, x_scale, w0, w1, out):
         w1_s = keep.tile([P, OUT_DIM], U8, name="w1_s", align_bytes=64)
         w1_g = keep.tile([P, OUT_DIM * 4], BF16, name="w1_g", align_bytes=64)
 
-        def transpose_weights(key):
-            words = state["w", key][:].bitcast(F32)
+        def transpose_weights(key, w_sb, row, first):
+            words = w_sb[:].bitcast(F32)
             bank = psum.tile([P, 2, 2, P], F32, name="bank2", tag="bank")
             for t in range(2):
                 for u in range(2):
-                    lo = 256 * t
+                    lo = row * t + first
                     nc.tensor.transpose(bank[:, t, u, :], words[:, lo + u : lo + 256 : 2], ident[:])
-            state[key] = bank
+            state["wbank", key] = bank
 
-        def weights_out(engine_copy, key, dst):
-            engine_copy(
+        def weights_out(key, dst):
+            nc.scalar.copy(
                 out=dst.bitcast(F32).rearrange("p (t m u) -> p t m u", t=2, u=2),
-                in_=state[key][:].rearrange("p t u m -> p t m u"),
+                in_=state["wbank", key][:].rearrange("p t u m -> p t m u"),
             )
 
         def quantize_w(src, codes, scales):
             nc.vector.quantize_mx(out=codes[:].bitcast(FP8X4), scales=scales[:], in_=src[:])
 
-        def widen(engine, u, g, c, first=0, last=None):
-            b, lo, n = u
+        def widen(engine, span, g, c, first=0, last=None):
+            n = span[1]
             last = last or 2 * n
-            values = state["x", u][:, g, c, first:last].bitcast(FP8)
-            tmp = new(("tmp", u), work, [P, G * 2 * 2 * n], BF16, "tmp")
+            values = state["x", span][:, g, c, first:last].bitcast(FP8)
+            tmp = new(("tmp", span), wide, [P, G * 2 * 2 * n], BF16, "tmp")
             row = (2 * g + c) * 2 * n
             dst = tmp[:, row + first : row + last]
             factor = sc[:, g, c : c + 1]
@@ -99,11 +107,10 @@ def tile_cnn_pa_t_kernel(tc, x_bytes, x_scale, w0, w1, out):
             else:
                 nc.vector.tensor_scalar(out=dst, in0=values, scalar1=factor, scalar2=None, op0=ALU.mult)
 
-        def interleave(b, pieces):
-            lo, n = pieces[0][1], pieces[0][2]
-            src = pieces[0] if ("tmp", pieces[0]) in state else (b, 0, Q)
-            first = lo - src[1]
-            grp = work.tile([P, len(pieces) * G * n * 4], BF16, name="grp", align_bytes=64)
+        def interleave(src, pieces):
+            n = pieces[0][1]
+            first = pieces[0][0] - src[0]
+            grp = wide.tile([P, len(pieces) * G * n * 4], BF16, name="grp", align_bytes=64)
             for j, u in enumerate(pieces):
                 state["grp", u] = grp[:, j * G * n * 4 : (j + 1) * G * n * 4]
             words = state["tmp", src][:].bitcast(F32).rearrange("p (g c q) -> p g c q", g=G, c=2)
@@ -113,231 +120,208 @@ def tile_cnn_pa_t_kernel(tc, x_bytes, x_scale, w0, w1, out):
                 in_=words.rearrange("p g c (h q) -> p h g q c", q=n),
             )
 
-        def quantize_x(u, g0=0, g1=G):
-            b, lo, n = u
+        def quantize_x(u):
+            n = u[1]
             codes = new(("xc", u), work, [P, G * n], U32, "xc")
             scales = new(("xs", u), work, [P, G * n], U8, "xs")
-            nc.vector.quantize_mx(
-                out=codes[:, g0 * n : g1 * n].bitcast(FP8X4),
-                scales=scales[:, g0 * n : g1 * n],
-                in_=state["grp", u][:, 4 * g0 * n : 4 * g1 * n],
-            )
+            nc.vector.quantize_mx(out=codes[:].bitcast(FP8X4), scales=scales[:], in_=state["grp", u])
 
         def layer1(u):
-            b, lo, n = u
-            bank = psum.tile([P, 2, n], F32, name="bank1", tag="bank")
-            for t in range(2):
-                for g in range(G):
-                    cols = slice(g * n, (g + 1) * n)
-                    wcols = slice(g * HID + t * P, g * HID + (t + 1) * P)
-                    nc.tensor.matmul_mx(
-                        out=bank[:, t, :],
-                        lhsT=w0_c[:, wcols].bitcast(FP8X4),
-                        lhsT_scale=w0_s[:, wcols],
-                        rhs=state["xc", u][:, cols].bitcast(FP8X4),
-                        rhs_scale=state["xs", u][:, cols],
-                        start=(g == 0),
-                        stop=(g == G - 1),
-                    )
-            state["bank1", b, lo] = bank
+            first, n = u
+            m = min(n, BANK_N)
+            for lo in range(0, n, m):
+                bank = psum.tile([P, 2, m], F32, name="bank1", tag="bank")
+                for t in range(2):
+                    for g in range(G):
+                        cols = slice(g * n + lo, g * n + lo + m)
+                        wcols = slice(g * HID + t * P, g * HID + (t + 1) * P)
+                        nc.tensor.matmul_mx(
+                            out=bank[:, t, :],
+                            lhsT=w0_c[:, wcols].bitcast(FP8X4),
+                            lhsT_scale=w0_s[:, wcols],
+                            rhs=state["xc", u][:, cols].bitcast(FP8X4),
+                            rhs_scale=state["xs", u][:, cols],
+                            start=(g == 0),
+                            stop=(g == G - 1),
+                        )
+                state["bank1", first + lo] = (bank, m)
 
-        def layer1_pass(u, g):
-            b, lo, n = u
-            if g == 0:
-                state["bank1", b, lo] = psum.tile([P, 2, n], F32, name="bank1", tag="bank")
-            for t in range(2):
-                cols = slice(g * n, (g + 1) * n)
-                wcols = slice(g * HID + t * P, g * HID + (t + 1) * P)
-                nc.tensor.matmul_mx(
-                    out=state["bank1", b, lo][:, t, :],
-                    lhsT=w0_c[:, wcols].bitcast(FP8X4),
-                    lhsT_scale=w0_s[:, wcols],
-                    rhs=state["xc", u][:, cols].bitcast(FP8X4),
-                    rhs_scale=state["xs", u][:, cols],
-                    start=(g == 0 and t == 0),
-                    stop=(g == G - 1 and t == 1),
-                )
-
-        def layer2_tile(engine, b, lo, n, t):
-            bank = psum.tile([P, n], F32, name="bank3", tag="bank")
-            wcols = slice(t * P, (t + 1) * P)
-            nc.tensor.matmul_mx(
-                out=bank[:],
-                lhsT=w1_c[:, wcols].bitcast(FP8X4),
-                lhsT_scale=w1_s[:, wcols],
-                rhs=state["hc", b][:, lo : lo + n].bitcast(FP8X4),
-                rhs_scale=state["hs", b][:, lo : lo + n],
-                start=True,
-                stop=True,
-            )
-            o_sb = outp.tile([P, n], F32, name="o_sb", tag="o_sb")
-            if engine == "S":
-                nc.scalar.activation(out=o_sb[:], in_=bank[:], func=ACT.Relu, scale=SCALE1)
-            else:
-                nc.vector.tensor_scalar(out=o_sb[:], in0=bank[:], scalar1=SCALE1, scalar2=0.0, op0=ALU.mult, op1=ALU.max)
-            nc.sync.dma_start(out=out[b].rearrange("(m t) r -> m t r", t=2)[:, t, lo : lo + n], in_=o_sb[:])
-
-        def hidden(engine, b, lo, n=BANK_N):
-            h = new(("h", b), work, [P, R * 4], BF16, "hgrp")
+        def hidden(engine, hspan, first):
+            bank, n = state["bank1", first]
+            h = new(("h", hspan), work, [P, 2 * hspan[1]], BF16, "hgrp")
+            lo = first - hspan[0]
             dst = h[:, 2 * lo : 2 * (lo + n)].rearrange("p (r c k) -> p r c k", c=2, k=2)
-            z = state["bank1", b, lo][:].rearrange("p c (r k) -> p r c k", k=2)
+            z = bank[:].rearrange("p c (r k) -> p r c k", k=2)
             if engine == "S":
                 nc.scalar.activation(out=dst, in_=z, func=ACT.Relu, scale=SCALE0)
             else:
                 nc.vector.tensor_scalar(out=dst, in0=z, scalar1=SCALE0, scalar2=0.0, op0=ALU.mult, op1=ALU.max)
 
-        def quantize_h(b, lo=0, n=R):
-            codes = new(("hc", b), work, [P, R], U32, "hc")
-            scales = new(("hs", b), work, [P, R], U8, "hs")
-            nc.vector.quantize_mx(
-                out=codes[:, lo : lo + n].bitcast(FP8X4),
-                scales=scales[:, lo : lo + n],
-                in_=state["h", b][:, 4 * lo : 4 * (lo + n)],
+        def quantize_h(hspan):
+            n = hspan[1] // 2
+            codes = new(("hc", hspan), work, [P, n], U32, "hc")
+            scales = new(("hs", hspan), work, [P, n], U8, "hs")
+            nc.vector.quantize_mx(out=codes[:].bitcast(FP8X4), scales=scales[:], in_=state["h", hspan][:])
+
+        def layer2_pass(dst, hspan, lo, n, t):
+            wcols = slice(t * P, (t + 1) * P)
+            nc.tensor.matmul_mx(
+                out=dst,
+                lhsT=w1_c[:, wcols].bitcast(FP8X4),
+                lhsT_scale=w1_s[:, wcols],
+                rhs=state["hc", hspan][:, lo : lo + n].bitcast(FP8X4),
+                rhs_scale=state["hs", hspan][:, lo : lo + n],
+                start=True,
+                stop=True,
             )
 
-        def layer2(b, lo=0, n=R):
-            bank = psum.tile([P, 2, n], F32, name="bank2", tag="bank")
-            for t in range(2):
-                wcols = slice(t * P, (t + 1) * P)
-                nc.tensor.matmul_mx(
-                    out=bank[:, t, :],
-                    lhsT=w1_c[:, wcols].bitcast(FP8X4),
-                    lhsT_scale=w1_s[:, wcols],
-                    rhs=state["hc", b][:, lo : lo + n].bitcast(FP8X4),
-                    rhs_scale=state["hs", b][:, lo : lo + n],
-                    start=True,
-                    stop=True,
-                )
-            state["bank2", b, lo] = bank
+        def layer2(hspan):
+            n = hspan[1] // 2
+            m = min(n, BANK_N)
+            for lo in range(0, n, m):
+                bank = psum.tile([P, 2, m], F32, name="bank2", tag="bank")
+                for t in range(2):
+                    layer2_pass(bank[:, t, :], hspan, lo, m, t)
+                state["bank2", hspan[0] + 2 * lo] = (bank, m)
 
-        def finish(engine, b, lo=0, n=R):
-            o_sb = outp.tile([P, 2, n], F32, name="o_sb", tag="o_sb")
-            bank = state["bank2", b, lo]
+        def scaled_relu(engine, dst, src):
             if engine == "S":
-                nc.scalar.activation(out=o_sb[:], in_=bank[:], func=ACT.Relu, scale=SCALE1)
+                nc.scalar.activation(out=dst, in_=src, func=ACT.Relu, scale=SCALE1)
             else:
-                nc.vector.tensor_scalar(out=o_sb[:], in0=bank[:], scalar1=SCALE1, scalar2=0.0, op0=ALU.mult, op1=ALU.max)
+                nc.vector.tensor_scalar(out=dst, in0=src, scalar1=SCALE1, scalar2=0.0, op0=ALU.mult, op1=ALU.max)
+
+        def finish(engine, first):
+            bank, n = state["bank2", first]
+            b, lo = divmod(first // 2, R)
+            o_sb = outp.tile([P, 2, n], F32, name="o_sb", tag="o_sb")
+            scaled_relu(engine, o_sb[:], bank[:])
             nc.sync.dma_start(out=out[b].rearrange("(m t) r -> m t r", t=2)[:, :, lo : lo + n], in_=o_sb[:])
 
+        def layer2_tile(engine, hspan, t):
+            n = hspan[1] // 2
+            b, lo = divmod(hspan[0] // 2, R)
+            bank = psum.tile([P, n], F32, name="bank3", tag="bank")
+            layer2_pass(bank[:], hspan, 0, n, t)
+            o_sb = outp.tile([P, n], F32, name="o_sb", tag="o_sb")
+            scaled_relu(engine, o_sb[:], bank[:])
+            nc.sync.dma_start(out=out[b].rearrange("(m t) r -> m t r", t=2)[:, t, lo : lo + n], in_=o_sb[:])
+
+        H = Q // 2
         LAST = BS - 1
-        EXTRA = 4
-        SHARE = 512
-        full = [(b, 0, Q) for b in range(BS)]
-        lower = [(b, 0, Q // 2) for b in range(BS)]
-        upper = [(b, Q // 2, Q // 2) for b in range(BS)]
-        a0, b0 = lower[0], upper[0]
-        a7, b7, c7 = lower[LAST], (LAST, Q // 2, Q // 4), (LAST, 3 * Q // 4, Q // 4)
-        load_x(a0)
-        load_x(b0)
-        load_x(full[1], 0, 1)
-        load_w(0, w0, 0)
-        load_x(full[1], 1, 2)
-        load_w(1, w0, 1)
-        load_x(full[2], 0, 1)
-        load_x(full[2], 1, 2)
-        load_w(2, w1, 0)
-        for b in range(3, BS):
-            load_x(full[b])
+        EXTRA, SHARE = 4, 1024
+        batch = [(b * Q, Q) for b in range(BS)]
+        lower = [(b * Q, H) for b in range(BS)]
+        upper = [(b * Q + H, H) for b in range(BS)]
+        a7, b7, c7 = lower[LAST], (LAST * Q + H, H // 2), (LAST * Q + H + H // 2, H // 2)
+        for g in range(G):
+            load_x(batch[0], g, 0, 1)
+            load_x(batch[0], g, 1, 2)
+        for g in range(G):
+            load_x(batch[1], g, 1, 2)
+            load_x(batch[1], g, 0, 1)
+        load_x(batch[2], 0)
+        load_x(batch[2], 1)
+        load_w(w0_sb, w0)
+        load_x(batch[3], 0)
+        load_x(batch[3], 1)
+        load_w(w1_sb, w1)
+        for b in range(4, BS):
+            load_batch(batch[b])
 
         warm = keep.tile([P, 1], F32, name="warm")
         nc.vector.memset(warm[:], 0.0)
         nc.scalar.activation(out=warm[:], in_=warm[:], func=ACT.Relu)
         ident = keep.tile([P, P], F32, name="ident")
         make_identity(nc, ident[:])
-        for key in range(3):
-            transpose_weights(key)
+        transpose_weights(0, w0_sb, 512, 0)
+        transpose_weights(1, w0_sb, 512, 256)
+        transpose_weights(2, w1_sb, 256, 0)
 
-        widen("V", a0, 0, 0)
-        widen("S", a0, 0, 1)
-        widen("V", a0, 1, 0)
-        widen("S", a0, 1, 1)
-        widen("V", b0, 0, 0)
-        widen("S", b0, 0, 1)
-        widen("V", b0, 1, 0)
-        widen("V", b0, 1, 1)
-        widen("S", full[1], 0, 1)
-        widen("S", full[1], 1, 1)
-        widen("S", full[2], 0, 1)
-        weights_out(nc.scalar.copy, 0, w0_g[:, 0 : HID * 4])
-        weights_out(nc.scalar.copy, 1, w0_g[:, HID * 4 :])
-        widen("S", full[2], 1, 1)
-        widen("S", full[3], 0, 1)
-        weights_out(nc.scalar.copy, 2, w1_g[:])
-        interleave(0, [a0])
-        widen("V", full[1], 0, 0)
-        quantize_x(a0)
-        interleave(0, [b0])
-        widen("V", full[1], 1, 0)
-        quantize_x(b0)
-        interleave(1, [lower[1], upper[1]])
-        widen("V", full[2], 0, 0)
-        widen("V", full[2], 1, 0)
+        def hidden_batch(b):
+            hidden("S", batch[b], lower[b][0])
+            hidden("S", batch[b], upper[b][0])
+
+        def multiply(u):
+            quantize_x(u)
+            layer1(u)
+
+        def second_layer(hspan):
+            quantize_h(hspan)
+            layer2(hspan)
+
+        widen("V", batch[0], 0, 0)
+        widen("S", batch[0], 0, 1)
+        widen("V", batch[0], 1, 0)
+        widen("V", batch[0], 1, 1)
+        widen("S", batch[1], 0, 1)
+        widen("S", batch[1], 1, 1)
+        widen("V", batch[1], 0, 0)
+        interleave(batch[0], [batch[0]])
+        widen("V", batch[1], 1, 0)
+        quantize_x(batch[0])
+        widen("S", batch[2], 0, 1)
+        widen("S", batch[2], 1, 1)
+        widen("S", batch[3], 0, 1)
+        weights_out(0, w0_g[:, 0 : HID * 4])
+        weights_out(1, w0_g[:, HID * 4 :])
+        interleave(batch[1], [batch[1]])
+        widen("V", batch[2], 0, 0)
+        widen("V", batch[2], 1, 0)
+        quantize_x(batch[1])
         quantize_w(w0_g, w0_c, w0_s)
-        layer1(a0)
-        layer1(b0)
-        quantize_x(lower[1])
-        layer1(lower[1])
-        for i in range(2, LAST):
-            late = i >= LAST - 2
+        layer1(batch[0])
+        layer1(batch[1])
+        widen("S", batch[3], 1, 1)
+        weights_out(2, w1_g[:])
+        widen("S", batch[4], 0, 1)
+        interleave(batch[2], [lower[2], upper[2]])
+        widen("V", batch[3], 0, 0)
+        multiply(lower[2])
+        widen("V", batch[3], 1, 0)
+        quantize_w(w1_g, w1_c, w1_s)
+        for i in range(3, LAST):
             if i < LAST - 1:
-                widen("S", full[i + 1], 1, 1)
+                widen("S", batch[i + 1], 1, 1)
+                if i == 3:
+                    hidden_batch(0)
                 if i + 1 == EXTRA:
-                    widen("S", full[i + 1], 1, 0, 0, SHARE)
-                hidden("S", i - 2, 0)
-                hidden("S", i - 2, BANK_N)
-            if not late:
-                widen("S", full[i + 2], 0, 1)
-            interleave(i, [lower[i], upper[i]])
-            quantize_x(upper[i - 1])
-            layer1(upper[i - 1])
-            widen("V", full[i + 1], 0, 0)
-            if i == 2:
-                quantize_w(w1_g, w1_c, w1_s)
-            elif i < LAST - 1:
-                quantize_h(i - 3)
-                layer2(i - 3)
-                if late:
-                    hidden("S", i - 1, 0)
-                    hidden("S", i - 1, BANK_N)
-                    widen("S", full[LAST], 0, 1)
-                    widen("S", full[LAST], 1, 1)
-                finish("S", i - 3)
-            else:
-                quantize_h(i - 3)
-                layer2(i - 3)
-                quantize_h(i - 2)
-                layer2(i - 2)
-                hidden("S", i - 1, 0)
-                hidden("S", i - 1, BANK_N)
-                finish("S", i - 3)
-            widen("V", full[i + 1], 1, 0, SHARE if i + 1 == EXTRA else 0)
-            quantize_x(lower[i])
-            layer1(lower[i])
-        interleave(LAST, [a7])
-        quantize_x(upper[LAST - 1])
-        layer1(upper[LAST - 1])
-        quantize_x(a7)
-        layer1(a7)
-        hidden("S", LAST - 1, 0)
-        finish("S", LAST - 3)
-        hidden("S", LAST - 1, BANK_N)
-        hidden("S", LAST, 0)
-        interleave(LAST, [b7, c7])
-        quantize_h(LAST - 2)
-        layer2(LAST - 2)
-        quantize_x(b7)
-        layer1(b7)
-        quantize_x(c7)
-        layer1(c7)
-        quantize_h(LAST - 1)
-        layer2(LAST - 1)
-        quantize_h(LAST, 0, R // 2)
-        layer2(LAST, 0, R // 2)
-        finish("S", LAST - 2)
-        hidden("V", LAST, b7[1], b7[2])
-        hidden("S", LAST, c7[1], c7[2])
-        quantize_h(LAST, R // 2, R // 2)
-        finish("S", LAST - 1)
-        finish("V", LAST, 0, R // 2)
-        layer2_tile("V", LAST, R // 2, R // 2, 0)
-        layer2_tile("S", LAST, R // 2, R // 2, 1)
+                    widen("S", batch[i + 1], 1, 0, 0, SHARE)
+                hidden_batch(i - 2)
+            if i < LAST - 2:
+                widen("S", batch[i + 2], 0, 1)
+            interleave(batch[i], [lower[i], upper[i]])
+            multiply(upper[i - 1])
+            widen("V", batch[i + 1], 0, 0)
+            second_layer(batch[i - 3])
+            if i == LAST - 2:
+                hidden_batch(i - 1)
+                widen("S", batch[LAST], 0, 1)
+                widen("S", batch[LAST], 1, 1)
+            if i == LAST - 1:
+                second_layer(batch[i - 2])
+                hidden_batch(i - 1)
+            finish("S", batch[i - 3][0])
+            if i + 1 != EXTRA or SHARE < D:
+                widen("V", batch[i + 1], 1, 0, SHARE if i + 1 == EXTRA else 0)
+            multiply(lower[i])
+        interleave(batch[LAST], [a7])
+        multiply(upper[6])
+        multiply(a7)
+        hidden("S", batch[6], lower[6][0])
+        finish("S", batch[4][0])
+        hidden("S", batch[6], upper[6][0])
+        hidden("S", a7, a7[0])
+        interleave(batch[LAST], [b7, c7])
+        second_layer(batch[5])
+        finish("S", batch[5][0])
+        multiply(b7)
+        multiply(c7)
+        second_layer(batch[6])
+        second_layer(a7)
+        hidden("V", upper[7], b7[0])
+        hidden("S", upper[7], c7[0])
+        finish("S", batch[6][0])
+        quantize_h(upper[7])
+        finish("V", a7[0])
+        layer2_tile("V", upper[7], 0)
+        layer2_tile("S", upper[7], 1)

@@ -107,24 +107,28 @@ def tile_cnn_pa_t_kernel(tc, x_bytes, x_scale, w0, w1, out):
             else:
                 nc.vector.tensor_scalar(out=dst, in0=values, scalar1=factor, scalar2=None, op0=ALU.mult)
 
-        def interleave(src, pieces):
+        def interleave(src, pieces, g0=0, g1=G):
             n = pieces[0][1]
             first = pieces[0][0] - src[0]
-            grp = wide.tile([P, len(pieces) * G * n * 4], BF16, name="grp", align_bytes=64)
+            grp = new(("grp_tile", pieces[0]), wide, [P, len(pieces) * G * n * 4], BF16, "grp")
             for j, u in enumerate(pieces):
                 state["grp", u] = grp[:, j * G * n * 4 : (j + 1) * G * n * 4]
             words = state["tmp", src][:].bitcast(F32).rearrange("p (g c q) -> p g c q", g=G, c=2)
             words = words[:, :, :, first : first + len(pieces) * n]
             nc.vector.tensor_copy(
-                out=grp[:].bitcast(F32).rearrange("p (h g q c) -> p h g q c", g=G, q=n, c=2),
-                in_=words.rearrange("p g c (h q) -> p h g q c", q=n),
+                out=grp[:].bitcast(F32).rearrange("p (h g q c) -> p h g q c", g=G, q=n, c=2)[:, :, g0:g1],
+                in_=words.rearrange("p g c (h q) -> p h g q c", q=n)[:, :, g0:g1],
             )
 
-        def quantize_x(u):
+        def quantize_x(u, g0=0, g1=G):
             n = u[1]
             codes = new(("xc", u), work, [P, G * n], U32, "xc")
             scales = new(("xs", u), work, [P, G * n], U8, "xs")
-            nc.vector.quantize_mx(out=codes[:].bitcast(FP8X4), scales=scales[:], in_=state["grp", u])
+            nc.vector.quantize_mx(
+                out=codes[:, g0 * n : g1 * n].bitcast(FP8X4),
+                scales=scales[:, g0 * n : g1 * n],
+                in_=state["grp", u][:, 4 * g0 * n : 4 * g1 * n],
+            )
 
         def layer1(u):
             first, n = u
@@ -208,7 +212,7 @@ def tile_cnn_pa_t_kernel(tc, x_bytes, x_scale, w0, w1, out):
 
         H = Q // 2
         LAST = BS - 1
-        EXTRA, SHARE = 4, 1024
+        SHARE = D // 4
         batch = [(b * Q, Q) for b in range(BS)]
         lower = [(b * Q, H) for b in range(BS)]
         upper = [(b * Q + H, H) for b in range(BS)]
@@ -216,16 +220,18 @@ def tile_cnn_pa_t_kernel(tc, x_bytes, x_scale, w0, w1, out):
         for g in range(G):
             load_x(batch[0], g, 0, 1)
             load_x(batch[0], g, 1, 2)
-        for g in range(G):
-            load_x(batch[1], g, 1, 2)
-            load_x(batch[1], g, 0, 1)
-        load_x(batch[2], 0)
-        load_x(batch[2], 1)
+        load_x(batch[1], 0, 0, 1)
+        load_x(batch[1], 0, 1, 2)
+        load_x(batch[1], 1, 1, 2)
+        load_x(batch[1], 1, 0, 1)
+        for b in (2, 3):
+            for g in range(G):
+                load_x(batch[b], g)
         load_w(w0_sb, w0)
-        load_x(batch[3], 0)
-        load_x(batch[3], 1)
+        for g in range(G):
+            load_x(batch[4], g)
         load_w(w1_sb, w1)
-        for b in range(4, BS):
+        for b in range(5, BS):
             load_batch(batch[b])
 
         warm = keep.tile([P, 1], F32, name="warm")
@@ -250,60 +256,77 @@ def tile_cnn_pa_t_kernel(tc, x_bytes, x_scale, w0, w1, out):
             layer2(hspan)
 
         widen("V", batch[0], 0, 0)
-        widen("S", batch[0], 0, 1)
+        widen("S", batch[0], 0, 1, 0, Q)
+        widen("V", batch[0], 0, 1, Q)
         widen("V", batch[0], 1, 0)
-        widen("V", batch[0], 1, 1)
+        widen("S", batch[0], 1, 1)
         widen("S", batch[1], 0, 1)
         widen("S", batch[1], 1, 1)
+        interleave(batch[0], [batch[0]], 0, 1)
         widen("V", batch[1], 0, 0)
-        interleave(batch[0], [batch[0]])
+        quantize_x(batch[0], 0, 1)
+        interleave(batch[0], [batch[0]], 1, 2)
         widen("V", batch[1], 1, 0)
-        quantize_x(batch[0])
-        widen("S", batch[2], 0, 1)
-        widen("S", batch[2], 1, 1)
-        widen("S", batch[3], 0, 1)
+        quantize_x(batch[0], 1, 2)
+        for b in (2, 3):
+            for g in range(G):
+                widen("S", batch[b], g, 1)
+        widen("S", batch[4], 0, 1)
         weights_out(0, w0_g[:, 0 : HID * 4])
         weights_out(1, w0_g[:, HID * 4 :])
+        widen("S", batch[4], 1, 1)
+        widen("S", batch[4], 1, 0, 0, SHARE)
+        weights_out(2, w1_g[:])
         interleave(batch[1], [batch[1]])
         widen("V", batch[2], 0, 0)
         widen("V", batch[2], 1, 0)
         quantize_x(batch[1])
-        quantize_w(w0_g, w0_c, w0_s)
-        layer1(batch[0])
-        layer1(batch[1])
-        widen("S", batch[3], 1, 1)
-        weights_out(2, w1_g[:])
-        widen("S", batch[4], 0, 1)
-        interleave(batch[2], [lower[2], upper[2]])
+        interleave(batch[2], [batch[2]])
         widen("V", batch[3], 0, 0)
-        multiply(lower[2])
         widen("V", batch[3], 1, 0)
+        quantize_x(batch[2])
+        quantize_w(w0_g, w0_c, w0_s)
+        for b in range(3):
+            layer1(batch[b])
+        widen("S", batch[5], 0, 1)
+        widen("S", batch[5], 1, 1)
+        hidden_batch(0)
+        hidden_batch(1)
+        interleave(batch[3], [batch[3]])
+        widen("V", batch[4], 0, 0)
         quantize_w(w1_g, w1_c, w1_s)
-        for i in range(3, LAST):
-            if i < LAST - 1:
-                widen("S", batch[i + 1], 1, 1)
-                if i == 3:
-                    hidden_batch(0)
-                if i + 1 == EXTRA:
-                    widen("S", batch[i + 1], 1, 0, 0, SHARE)
-                hidden_batch(i - 2)
-            if i < LAST - 2:
-                widen("S", batch[i + 2], 0, 1)
-            interleave(batch[i], [lower[i], upper[i]])
-            multiply(upper[i - 1])
-            widen("V", batch[i + 1], 0, 0)
-            second_layer(batch[i - 3])
-            if i == LAST - 2:
-                hidden_batch(i - 1)
-                widen("S", batch[LAST], 0, 1)
-                widen("S", batch[LAST], 1, 1)
-            if i == LAST - 1:
-                second_layer(batch[i - 2])
-                hidden_batch(i - 1)
-            finish("S", batch[i - 3][0])
-            if i + 1 != EXTRA or SHARE < D:
-                widen("V", batch[i + 1], 1, 0, SHARE if i + 1 == EXTRA else 0)
-            multiply(lower[i])
+        widen("V", batch[4], 1, 0, SHARE)
+        multiply(batch[3])
+        widen("S", batch[6], 0, 1)
+        hidden_batch(2)
+        interleave(batch[4], [batch[4]])
+        widen("V", batch[5], 0, 0)
+        second_layer(batch[0])
+        widen("V", batch[5], 1, 0)
+        second_layer(batch[1])
+        finish("S", batch[0][0])
+        multiply(batch[4])
+        widen("S", batch[6], 1, 1)
+        hidden_batch(3)
+        finish("S", batch[1][0])
+        interleave(batch[5], [lower[5], upper[5]])
+        widen("V", batch[6], 0, 0)
+        second_layer(batch[2])
+        hidden_batch(4)
+        widen("S", batch[LAST], 0, 1)
+        widen("S", batch[LAST], 1, 1)
+        finish("S", batch[2][0])
+        widen("V", batch[6], 1, 0)
+        multiply(lower[5])
+        interleave(batch[6], [lower[6], upper[6]])
+        multiply(upper[5])
+        widen("V", batch[LAST], 0, 0)
+        second_layer(batch[3])
+        second_layer(batch[4])
+        hidden_batch(5)
+        finish("S", batch[3][0])
+        widen("V", batch[LAST], 1, 0)
+        multiply(lower[6])
         interleave(batch[LAST], [a7])
         multiply(upper[6])
         multiply(a7)

@@ -10,6 +10,10 @@ Q = D // 2
 R = Q // 2
 G = 2
 BANK_N = 256
+PASS_WORDS = 256
+
+SHARE = D // 4
+SHARED_BATCH = 4
 
 FLOPS = 2 * BS * Q * HID * (2 * CIN) + 2 * BS * R * OUT_DIM * (2 * HID)
 
@@ -31,37 +35,26 @@ def tile_cnn_pa_t_kernel(tc, x_bytes, x_scale, w0, w1, out):
 
     with ExitStack() as ctx:
         keep = ctx.enter_context(tc.tile_pool(name="keep", bufs=1))
-        outp = ctx.enter_context(tc.tile_pool(name="outp", bufs=6))
+        outp = ctx.enter_context(tc.tile_pool(name="outp", bufs=8))
         wide = ctx.enter_context(tc.tile_pool(name="wide", bufs=5))
         work = ctx.enter_context(tc.tile_pool(name="work", bufs=5))
         psum = ctx.enter_context(tc.psum_pool(name="psum", bufs=8))
         ctx.enter_context(tc.manual_schedule())
 
-        state = {}
+        tiles = {}
 
-        def new(key, pool, shape, dtype, name):
-            if key not in state:
-                state[key] = pool.tile(shape, dtype, name=name, align_bytes=64)
-            return state[key]
+        def tile_of(key, pool, shape, dtype, name):
+            if key not in tiles:
+                tiles[key] = pool.tile(shape, dtype, name=name, align_bytes=64)
+            return tiles[key]
 
-        sc = keep.tile([P, G, 8], F32, name="sc")
-        nc.scalar.dma_start(out=sc[:, :, 0:2], in_=x_scale.rearrange("o (g p c) x -> p g (o c x)", g=G, p=P, c=2))
-        xv = x_bytes.rearrange("b (g p c) d -> p g c b d", g=G, p=P, c=2)
+        scale_sb = keep.tile([P, G, 8], F32, name="scale_sb")
+        nc.scalar.dma_start(out=scale_sb[:, :, 0:2], in_=x_scale.rearrange("o (g p s) x -> p g (o s x)", g=G, p=P, s=2))
+        x_rows = x_bytes.rearrange("b (g p s) d -> p g s b d", g=G, p=P, s=2)
 
-        def load_x(span, g, c0=0, c1=2):
-            first, n = span
-            x_t = new(("x", span), keep, [P, G, 2, 2 * n], U8, "x_%d" % first)
-            b, lo = divmod(first, Q)
-            if n <= Q:
-                nc.sync.dma_start(out=x_t[:, g, c0:c1], in_=xv[:, g, c0:c1, b, 2 * lo : 2 * (lo + n)])
-            else:
-                for c in range(c0, c1):
-                    rows = x_t[:, g, c].rearrange("p (b d) -> p b d", d=D)
-                    nc.sync.dma_start(out=rows, in_=xv[:, g, c, b : b + n // Q])
-
-        def load_batch(span):
-            x_t = new(("x", span), keep, [P, G, 2, D], U8, "x_%d" % span[0])
-            nc.sync.dma_start(out=x_t[:], in_=xv[:, :, :, span[0] // Q])
+        def load_x(b, passes, slots):
+            x_sb = tile_of(("x", b), keep, [P, G, 2, D], U8, "x_%d" % b)
+            nc.sync.dma_start(out=x_sb[:, passes, slots], in_=x_rows[:, passes, slots, b])
 
         w0_sb = keep.tile([P, 2 * 2 * CIN], BF16, name="w0_sb", align_bytes=64)
         w1_sb = keep.tile([P, 2 * 2 * HID], BF16, name="w1_sb", align_bytes=64)
@@ -69,282 +62,278 @@ def tile_cnn_pa_t_kernel(tc, x_bytes, x_scale, w0, w1, out):
         def load_w(w_sb, w):
             nc.sync.dma_start(out=w_sb[:], in_=w.rearrange("(m t) c k -> m (t c k)", t=2))
 
-        w0_c = keep.tile([P, G * HID], U32, name="w0_c", align_bytes=64)
-        w0_s = keep.tile([P, G * HID], U8, name="w0_s", align_bytes=64)
-        w0_g = keep.tile([P, G * HID * 4], BF16, name="w0_g", align_bytes=64)
-        w1_c = keep.tile([P, OUT_DIM], U32, name="w1_c", align_bytes=64)
-        w1_s = keep.tile([P, OUT_DIM], U8, name="w1_s", align_bytes=64)
-        w1_g = keep.tile([P, OUT_DIM * 4], BF16, name="w1_g", align_bytes=64)
+        w0_codes = keep.tile([P, G * HID], U32, name="w0_codes", align_bytes=64)
+        w0_scales = keep.tile([P, G * HID], U8, name="w0_scales", align_bytes=64)
+        w0_grouped = keep.tile([P, G * HID * 4], BF16, name="w0_grouped", align_bytes=64)
+        w1_codes = keep.tile([P, OUT_DIM], U32, name="w1_codes", align_bytes=64)
+        w1_scales = keep.tile([P, OUT_DIM], U8, name="w1_scales", align_bytes=64)
+        w1_grouped = keep.tile([P, OUT_DIM * 4], BF16, name="w1_grouped", align_bytes=64)
 
-        def transpose_weights(key, w_sb, row, first):
+        def transpose_weights(w_sb, passes, g):
             words = w_sb[:].bitcast(F32)
-            bank = psum.tile([P, 2, 2, P], F32, name="bank2", tag="bank")
+            bank = psum.tile([P, 2, 2, P], F32, name="weight_bank", tag="bank")
             for t in range(2):
-                for u in range(2):
-                    lo = row * t + first
-                    nc.tensor.transpose(bank[:, t, u, :], words[:, lo + u : lo + 256 : 2], ident[:])
-            state["wbank", key] = bank
+                for s in range(2):
+                    lo = (passes * t + g) * PASS_WORDS
+                    nc.tensor.transpose(bank[:, t, s, :], words[:, lo + s : lo + PASS_WORDS : 2], ident[:])
+            return bank
 
-        def weights_out(key, dst):
+        def weights_out(bank, dst):
             nc.scalar.copy(
-                out=dst.bitcast(F32).rearrange("p (t m u) -> p t m u", t=2, u=2),
-                in_=state["wbank", key][:].rearrange("p t u m -> p t m u"),
+                out=dst.bitcast(F32).rearrange("p (t m s) -> p t m s", t=2, s=2),
+                in_=bank[:].rearrange("p t s m -> p t m s"),
             )
 
-        def quantize_w(src, codes, scales):
-            nc.vector.quantize_mx(out=codes[:].bitcast(FP8X4), scales=scales[:], in_=src[:])
+        def quantize_w(grouped, codes, scales):
+            nc.vector.quantize_mx(out=codes[:].bitcast(FP8X4), scales=scales[:], in_=grouped[:])
 
-        def widen(engine, span, g, c, first=0, last=None):
-            n = span[1]
-            last = last or 2 * n
-            values = state["x", span][:, g, c, first:last].bitcast(FP8)
-            tmp = new(("tmp", span), wide, [P, G * 2 * 2 * n], BF16, "tmp")
-            row = (2 * g + c) * 2 * n
-            dst = tmp[:, row + first : row + last]
-            factor = sc[:, g, c : c + 1]
+        def widen(engine, b, g, s, first=0, last=D):
+            values = tiles["x", b][:, g, s, first:last].bitcast(FP8)
+            widened = tile_of(("widened", b), wide, [P, G * 2 * D], BF16, "widened")
+            row = (2 * g + s) * D
+            dst = widened[:, row + first : row + last]
+            factor = scale_sb[:, g, s : s + 1]
             if engine == "S":
                 nc.scalar.activation(out=dst, in_=values, func=ACT.Copy, scale=factor)
             else:
                 nc.vector.tensor_scalar(out=dst, in0=values, scalar1=factor, scalar2=None, op0=ALU.mult)
 
-        def interleave(src, pieces, g0=0, g1=G):
+        def interleave(pieces, g0=0, g1=G):
             n = pieces[0][1]
-            first = pieces[0][0] - src[0]
-            grp = new(("grp_tile", pieces[0]), wide, [P, len(pieces) * G * n * 4], BF16, "grp")
-            for j, u in enumerate(pieces):
-                state["grp", u] = grp[:, j * G * n * 4 : (j + 1) * G * n * 4]
-            words = state["tmp", src][:].bitcast(F32).rearrange("p (g c q) -> p g c q", g=G, c=2)
+            b, first = divmod(pieces[0][0], Q)
+            grouped = tile_of(("grouped_tile", pieces[0]), wide, [P, len(pieces) * G * n * 4], BF16, "grouped")
+            for i, piece in enumerate(pieces):
+                tiles["grouped", piece] = grouped[:, i * G * n * 4 : (i + 1) * G * n * 4]
+            words = tiles["widened", b][:].bitcast(F32).rearrange("p (g s q) -> p g s q", g=G, s=2)
             words = words[:, :, :, first : first + len(pieces) * n]
             nc.vector.tensor_copy(
-                out=grp[:].bitcast(F32).rearrange("p (h g q c) -> p h g q c", g=G, q=n, c=2)[:, :, g0:g1],
-                in_=words.rearrange("p g c (h q) -> p h g q c", q=n)[:, :, g0:g1],
+                out=grouped[:].bitcast(F32).rearrange("p (i g q s) -> p i g q s", g=G, q=n, s=2)[:, :, g0:g1],
+                in_=words.rearrange("p g s (i q) -> p i g q s", q=n)[:, :, g0:g1],
             )
 
-        def quantize_x(u, g0=0, g1=G):
-            n = u[1]
-            codes = new(("xc", u), work, [P, G * n], U32, "xc")
-            scales = new(("xs", u), work, [P, G * n], U8, "xs")
+        def quantize_x(span, g0=0, g1=G):
+            n = span[1]
+            codes = tile_of(("x_codes", span), work, [P, G * n], U32, "x_codes")
+            scales = tile_of(("x_scales", span), work, [P, G * n], U8, "x_scales")
             nc.vector.quantize_mx(
                 out=codes[:, g0 * n : g1 * n].bitcast(FP8X4),
                 scales=scales[:, g0 * n : g1 * n],
-                in_=state["grp", u][:, 4 * g0 * n : 4 * g1 * n],
+                in_=tiles["grouped", span][:, 4 * g0 * n : 4 * g1 * n],
             )
 
-        def layer1(u):
-            first, n = u
-            m = min(n, BANK_N)
-            for lo in range(0, n, m):
-                bank = psum.tile([P, 2, m], F32, name="bank1", tag="bank")
+        def layer1(span):
+            first, n = span
+            width = min(n, BANK_N)
+            for lo in range(0, n, width):
+                bank = psum.tile([P, 2, width], F32, name="hidden_bank", tag="bank")
                 for t in range(2):
                     for g in range(G):
-                        cols = slice(g * n + lo, g * n + lo + m)
-                        wcols = slice(g * HID + t * P, g * HID + (t + 1) * P)
+                        cols = slice(g * n + lo, g * n + lo + width)
+                        w_cols = slice(g * HID + t * P, g * HID + (t + 1) * P)
                         nc.tensor.matmul_mx(
                             out=bank[:, t, :],
-                            lhsT=w0_c[:, wcols].bitcast(FP8X4),
-                            lhsT_scale=w0_s[:, wcols],
-                            rhs=state["xc", u][:, cols].bitcast(FP8X4),
-                            rhs_scale=state["xs", u][:, cols],
+                            lhsT=w0_codes[:, w_cols].bitcast(FP8X4),
+                            lhsT_scale=w0_scales[:, w_cols],
+                            rhs=tiles["x_codes", span][:, cols].bitcast(FP8X4),
+                            rhs_scale=tiles["x_scales", span][:, cols],
                             start=(g == 0),
                             stop=(g == G - 1),
                         )
-                state["bank1", first + lo] = (bank, m)
+                tiles["hidden_bank", first + lo] = (bank, width)
 
-        def hidden(engine, hspan, first):
-            bank, n = state["bank1", first]
-            h = new(("h", hspan), work, [P, 2 * hspan[1]], BF16, "hgrp")
-            lo = first - hspan[0]
-            dst = h[:, 2 * lo : 2 * (lo + n)].rearrange("p (r c k) -> p r c k", c=2, k=2)
-            z = bank[:].rearrange("p c (r k) -> p r c k", k=2)
+        def scaled_relu(engine, dst, src, factor):
             if engine == "S":
-                nc.scalar.activation(out=dst, in_=z, func=ACT.Relu, scale=SCALE0)
+                nc.scalar.activation(out=dst, in_=src, func=ACT.Relu, scale=factor)
             else:
-                nc.vector.tensor_scalar(out=dst, in0=z, scalar1=SCALE0, scalar2=0.0, op0=ALU.mult, op1=ALU.max)
+                nc.vector.tensor_scalar(out=dst, in0=src, scalar1=factor, scalar2=0.0, op0=ALU.mult, op1=ALU.max)
 
-        def quantize_h(hspan):
-            n = hspan[1] // 2
-            codes = new(("hc", hspan), work, [P, n], U32, "hc")
-            scales = new(("hs", hspan), work, [P, n], U8, "hs")
-            nc.vector.quantize_mx(out=codes[:].bitcast(FP8X4), scales=scales[:], in_=state["h", hspan][:])
+        def hidden(engine, h_span, first):
+            bank, width = tiles["hidden_bank", first]
+            h = tile_of(("h", h_span), work, [P, 2 * h_span[1]], BF16, "h")
+            lo = first - h_span[0]
+            dst = h[:, 2 * lo : 2 * (lo + width)].rearrange("p (r s k) -> p r s k", s=2, k=2)
+            scaled_relu(engine, dst, bank[:].rearrange("p s (r k) -> p r s k", k=2), SCALE0)
 
-        def layer2_pass(dst, hspan, lo, n, t):
-            wcols = slice(t * P, (t + 1) * P)
+        def quantize_h(h_span):
+            n = h_span[1] // 2
+            codes = tile_of(("h_codes", h_span), work, [P, n], U32, "h_codes")
+            scales = tile_of(("h_scales", h_span), work, [P, n], U8, "h_scales")
+            nc.vector.quantize_mx(out=codes[:].bitcast(FP8X4), scales=scales[:], in_=tiles["h", h_span][:])
+
+        def layer2_pass(dst, h_span, lo, width, t):
+            w_cols = slice(t * P, (t + 1) * P)
             nc.tensor.matmul_mx(
                 out=dst,
-                lhsT=w1_c[:, wcols].bitcast(FP8X4),
-                lhsT_scale=w1_s[:, wcols],
-                rhs=state["hc", hspan][:, lo : lo + n].bitcast(FP8X4),
-                rhs_scale=state["hs", hspan][:, lo : lo + n],
+                lhsT=w1_codes[:, w_cols].bitcast(FP8X4),
+                lhsT_scale=w1_scales[:, w_cols],
+                rhs=tiles["h_codes", h_span][:, lo : lo + width].bitcast(FP8X4),
+                rhs_scale=tiles["h_scales", h_span][:, lo : lo + width],
                 start=True,
                 stop=True,
             )
 
-        def layer2(hspan):
-            n = hspan[1] // 2
-            m = min(n, BANK_N)
-            for lo in range(0, n, m):
-                bank = psum.tile([P, 2, m], F32, name="bank2", tag="bank")
+        def layer2(h_span):
+            n = h_span[1] // 2
+            width = min(n, BANK_N)
+            for lo in range(0, n, width):
+                bank = psum.tile([P, 2, width], F32, name="out_bank", tag="bank")
                 for t in range(2):
-                    layer2_pass(bank[:, t, :], hspan, lo, m, t)
-                state["bank2", hspan[0] + 2 * lo] = (bank, m)
+                    layer2_pass(bank[:, t, :], h_span, lo, width, t)
+                tiles["out_bank", h_span[0] + 2 * lo] = (bank, width)
 
-        def scaled_relu(engine, dst, src):
-            if engine == "S":
-                nc.scalar.activation(out=dst, in_=src, func=ACT.Relu, scale=SCALE1)
-            else:
-                nc.vector.tensor_scalar(out=dst, in0=src, scalar1=SCALE1, scalar2=0.0, op0=ALU.mult, op1=ALU.max)
-
-        def finish(engine, first):
-            bank, n = state["bank2", first]
+        def out_rows(first, width):
             b, lo = divmod(first // 2, R)
-            o_sb = outp.tile([P, 2, n], F32, name="o_sb", tag="o_sb")
-            scaled_relu(engine, o_sb[:], bank[:])
-            nc.sync.dma_start(out=out[b].rearrange("(m t) r -> m t r", t=2)[:, :, lo : lo + n], in_=o_sb[:])
+            return out[b].rearrange("(m t) r -> m t r", t=2)[:, :, lo : lo + width]
 
-        def layer2_tile(engine, hspan, t):
-            n = hspan[1] // 2
-            b, lo = divmod(hspan[0] // 2, R)
-            bank = psum.tile([P, n], F32, name="bank3", tag="bank")
-            layer2_pass(bank[:], hspan, 0, n, t)
-            o_sb = outp.tile([P, n], F32, name="o_sb", tag="o_sb")
-            scaled_relu(engine, o_sb[:], bank[:])
-            nc.sync.dma_start(out=out[b].rearrange("(m t) r -> m t r", t=2)[:, t, lo : lo + n], in_=o_sb[:])
+        def finish(engine, span):
+            bank, width = tiles["out_bank", span[0]]
+            o_sb = outp.tile([P, 2, width], F32, name="o_sb", tag="o_sb")
+            scaled_relu(engine, o_sb[:], bank[:], SCALE1)
+            nc.sync.dma_start(out=out_rows(span[0], width), in_=o_sb[:])
 
-        H = Q // 2
-        LAST = BS - 1
-        SHARE = D // 4
+        def finish_tile(engine, span, src, t):
+            width = span[1] // 2
+            o_sb = outp.tile([P, width], F32, name="o_sb", tag="o_sb")
+            scaled_relu(engine, o_sb[:], src, SCALE1)
+            nc.sync.dma_start(out=out_rows(span[0], width)[:, t], in_=o_sb[:])
+
         batch = [(b * Q, Q) for b in range(BS)]
-        lower = [(b * Q, H) for b in range(BS)]
-        upper = [(b * Q + H, H) for b in range(BS)]
-        a7, b7, c7 = lower[LAST], (LAST * Q + H, H // 2), (LAST * Q + H + H // 2, H // 2)
-        for g in range(G):
-            load_x(batch[0], g, 0, 1)
-            load_x(batch[0], g, 1, 2)
-        load_x(batch[1], 0, 0, 1)
-        load_x(batch[1], 0, 1, 2)
-        load_x(batch[1], 1, 1, 2)
-        load_x(batch[1], 1, 0, 1)
-        for b in (2, 3):
-            for g in range(G):
-                load_x(batch[b], g)
-        load_w(w0_sb, w0)
-        for g in range(G):
-            load_x(batch[4], g)
-        load_w(w1_sb, w1)
-        for b in range(5, BS):
-            load_batch(batch[b])
-
-        warm = keep.tile([P, 1], F32, name="warm")
-        nc.vector.memset(warm[:], 0.0)
-        nc.scalar.activation(out=warm[:], in_=warm[:], func=ACT.Relu)
-        ident = keep.tile([P, P], F32, name="ident")
-        make_identity(nc, ident[:])
-        transpose_weights(0, w0_sb, 512, 0)
-        transpose_weights(1, w0_sb, 512, 256)
-        transpose_weights(2, w1_sb, 256, 0)
+        lower = [(b * Q, BANK_N) for b in range(BS)]
+        upper = [(b * Q + BANK_N, BANK_N) for b in range(BS)]
+        third, fourth = (upper[7][0], BANK_N // 2), (upper[7][0] + BANK_N // 2, BANK_N // 2)
 
         def hidden_batch(b):
             hidden("S", batch[b], lower[b][0])
             hidden("S", batch[b], upper[b][0])
 
-        def multiply(u):
-            quantize_x(u)
-            layer1(u)
+        def first_layer(span):
+            quantize_x(span)
+            layer1(span)
 
-        def second_layer(hspan):
-            quantize_h(hspan)
-            layer2(hspan)
+        def second_layer(h_span):
+            quantize_h(h_span)
+            layer2(h_span)
 
-        widen("V", batch[0], 0, 0)
-        widen("S", batch[0], 0, 1, 0, Q)
-        widen("V", batch[0], 0, 1, Q)
-        widen("V", batch[0], 1, 0)
-        widen("S", batch[0], 1, 1)
-        widen("S", batch[1], 0, 1)
-        widen("S", batch[1], 1, 1)
-        interleave(batch[0], [batch[0]], 0, 1)
-        widen("V", batch[1], 0, 0)
-        quantize_x(batch[0], 0, 1)
-        interleave(batch[0], [batch[0]], 1, 2)
-        widen("V", batch[1], 1, 0)
-        quantize_x(batch[0], 1, 2)
+        both = slice(0, 2)
+        for b, g, s in ((0, 0, 0), (0, 0, 1), (0, 1, 0), (0, 1, 1), (1, 0, 0), (1, 0, 1), (1, 1, 1), (1, 1, 0)):
+            load_x(b, g, slice(s, s + 1))
         for b in (2, 3):
             for g in range(G):
-                widen("S", batch[b], g, 1)
-        widen("S", batch[4], 0, 1)
-        weights_out(0, w0_g[:, 0 : HID * 4])
-        weights_out(1, w0_g[:, HID * 4 :])
-        widen("S", batch[4], 1, 1)
-        widen("S", batch[4], 1, 0, 0, SHARE)
-        weights_out(2, w1_g[:])
-        interleave(batch[1], [batch[1]])
-        widen("V", batch[2], 0, 0)
-        widen("V", batch[2], 1, 0)
-        quantize_x(batch[1])
-        interleave(batch[2], [batch[2]])
-        widen("V", batch[3], 0, 0)
-        widen("V", batch[3], 1, 0)
-        quantize_x(batch[2])
-        quantize_w(w0_g, w0_c, w0_s)
+                load_x(b, g, both)
+        load_w(w0_sb, w0)
+        for g in range(G):
+            load_x(4, g, both)
+        load_w(w1_sb, w1)
+        for b in range(5, BS):
+            load_x(b, both, both)
+
+        warm = keep.tile([P, 1], F32, name="warm")
+        nc.vector.memset(warm[:], 0.0)
+        nc.scalar.activation(out=warm[:], in_=warm[:], func=ACT.Relu)
+
+        ident = keep.tile([P, P], F32, name="ident")
+        make_identity(nc, ident[:])
+        w0_banks = [transpose_weights(w0_sb, G, g) for g in range(G)]
+        w1_bank = transpose_weights(w1_sb, 1, 0)
+
+
+        widen("V", 0, 0, 0)
+        widen("S", 0, 0, 1, 0, D // 2)
+        widen("V", 0, 0, 1, D // 2)
+        widen("V", 0, 1, 0)
+        widen("S", 0, 1, 1)
+        for g in range(G):
+            widen("S", 1, g, 1)
+        for g in range(G):
+            interleave([batch[0]], g, g + 1)
+            widen("V", 1, g, 0)
+            quantize_x(batch[0], g, g + 1)
+
+        for b in (2, 3):
+            for g in range(G):
+                widen("S", b, g, 1)
+        widen("S", 4, 0, 1)
+        for g in range(G):
+            weights_out(w0_banks[g], w0_grouped[:, g * HID * 4 : (g + 1) * HID * 4])
+        widen("S", 4, 1, 1)
+        widen("S", SHARED_BATCH, 1, 0, 0, SHARE)
+        weights_out(w1_bank, w1_grouped[:])
+
+        for b in (1, 2):
+            interleave([batch[b]])
+            for g in range(G):
+                widen("V", b + 1, g, 0)
+            quantize_x(batch[b])
+        quantize_w(w0_grouped, w0_codes, w0_scales)
         for b in range(3):
             layer1(batch[b])
-        widen("S", batch[5], 0, 1)
-        widen("S", batch[5], 1, 1)
+
+        for g in range(G):
+            widen("S", 5, g, 1)
         hidden_batch(0)
         hidden_batch(1)
-        interleave(batch[3], [batch[3]])
-        widen("V", batch[4], 0, 0)
-        quantize_w(w1_g, w1_c, w1_s)
-        widen("V", batch[4], 1, 0, SHARE)
-        multiply(batch[3])
-        widen("S", batch[6], 0, 1)
+        interleave([lower[3], upper[3]])
+        widen("V", 4, 0, 0)
+        quantize_w(w1_grouped, w1_codes, w1_scales)
+        widen("V", SHARED_BATCH, 1, 0, SHARE)
+        first_layer(lower[3])
+
+        widen("S", 6, 0, 1)
         hidden_batch(2)
-        interleave(batch[4], [batch[4]])
-        widen("V", batch[5], 0, 0)
-        second_layer(batch[0])
-        widen("V", batch[5], 1, 0)
-        second_layer(batch[1])
-        finish("S", batch[0][0])
-        multiply(batch[4])
-        widen("S", batch[6], 1, 1)
+        interleave([lower[4], upper[4]])
+        first_layer(upper[3])
+        for g in range(G):
+            widen("V", 5, g, 0)
+            second_layer(batch[g])
+        finish("S", batch[0])
+        first_layer(lower[4])
+
+        widen("S", 6, 1, 1)
         hidden_batch(3)
-        finish("S", batch[1][0])
-        interleave(batch[5], [lower[5], upper[5]])
-        widen("V", batch[6], 0, 0)
+        finish("S", batch[1])
+        interleave([lower[5], upper[5]])
+        first_layer(upper[4])
+        widen("V", 6, 0, 0)
         second_layer(batch[2])
         hidden_batch(4)
-        widen("S", batch[LAST], 0, 1)
-        widen("S", batch[LAST], 1, 1)
-        finish("S", batch[2][0])
-        widen("V", batch[6], 1, 0)
-        multiply(lower[5])
-        interleave(batch[6], [lower[6], upper[6]])
-        multiply(upper[5])
-        widen("V", batch[LAST], 0, 0)
+        for g in range(G):
+            widen("S", 7, g, 1)
+        finish("S", batch[2])
+        widen("V", 6, 1, 0)
+        first_layer(lower[5])
+
+        interleave([lower[6], upper[6]])
+        first_layer(upper[5])
+        widen("V", 7, 0, 0)
         second_layer(batch[3])
         second_layer(batch[4])
         hidden_batch(5)
-        finish("S", batch[3][0])
-        widen("V", batch[LAST], 1, 0)
-        multiply(lower[6])
-        interleave(batch[LAST], [a7])
-        multiply(upper[6])
-        multiply(a7)
+        finish("S", batch[3])
+        widen("V", 7, 1, 0)
+        first_layer(lower[6])
+
+        interleave([lower[7]])
+        first_layer(upper[6])
+        first_layer(lower[7])
         hidden("S", batch[6], lower[6][0])
-        finish("S", batch[4][0])
+        finish("S", batch[4])
         hidden("S", batch[6], upper[6][0])
-        hidden("S", a7, a7[0])
-        interleave(batch[LAST], [b7, c7])
+        hidden("S", lower[7], lower[7][0])
+        interleave([third, fourth])
         second_layer(batch[5])
-        finish("S", batch[5][0])
-        multiply(b7)
-        multiply(c7)
+        finish("S", batch[5])
+        first_layer(third)
+        first_layer(fourth)
+
         second_layer(batch[6])
-        second_layer(a7)
-        hidden("V", upper[7], b7[0])
-        hidden("S", upper[7], c7[0])
-        finish("S", batch[6][0])
+        second_layer(lower[7])
+        hidden("V", upper[7], third[0])
+        hidden("S", upper[7], fourth[0])
+        for t in range(2):
+            finish_tile("S", batch[6], tiles["out_bank", batch[6][0]][0][:, t, :], t)
         quantize_h(upper[7])
-        finish("V", a7[0])
-        layer2_tile("V", upper[7], 0)
-        layer2_tile("S", upper[7], 1)
+        finish("V", lower[7])
+        for t, engine in enumerate("VS"):
+            bank = psum.tile([P, upper[7][1] // 2], F32, name="last_bank", tag="bank")
+            layer2_pass(bank[:], upper[7], 0, upper[7][1] // 2, t)
+            finish_tile(engine, upper[7], bank[:], t)

@@ -12,8 +12,9 @@ G = 2
 BANK_N = 256
 PASS_WORDS = 256
 
-SHARE = D // 4
+SHARE = 512
 SHARED_BATCH = 4
+FIRST_SPLITS = (768, 768, 768)
 
 FLOPS = 2 * BS * Q * HID * (2 * CIN) + 2 * BS * R * OUT_DIM * (2 * HID)
 
@@ -121,6 +122,19 @@ def tile_cnn_pa_t_kernel(tc, x_bytes, x_scale, w0, w1, out):
                 in_=tiles["grouped", span][:, 4 * g0 * n : 4 * g1 * n],
             )
 
+        def layer1_pass(dst, span, lo, width, t, g, start, stop):
+            cols = slice(g * span[1] + lo, g * span[1] + lo + width)
+            w_cols = slice(g * HID + t * P, g * HID + (t + 1) * P)
+            nc.tensor.matmul_mx(
+                out=dst,
+                lhsT=w0_codes[:, w_cols].bitcast(FP8X4),
+                lhsT_scale=w0_scales[:, w_cols],
+                rhs=tiles["x_codes", span][:, cols].bitcast(FP8X4),
+                rhs_scale=tiles["x_scales", span][:, cols],
+                start=start,
+                stop=stop,
+            )
+
         def layer1(span):
             first, n = span
             width = min(n, BANK_N)
@@ -128,17 +142,7 @@ def tile_cnn_pa_t_kernel(tc, x_bytes, x_scale, w0, w1, out):
                 bank = psum.tile([P, 2, width], F32, name="hidden_bank", tag="bank")
                 for t in range(2):
                     for g in range(G):
-                        cols = slice(g * n + lo, g * n + lo + width)
-                        w_cols = slice(g * HID + t * P, g * HID + (t + 1) * P)
-                        nc.tensor.matmul_mx(
-                            out=bank[:, t, :],
-                            lhsT=w0_codes[:, w_cols].bitcast(FP8X4),
-                            lhsT_scale=w0_scales[:, w_cols],
-                            rhs=tiles["x_codes", span][:, cols].bitcast(FP8X4),
-                            rhs_scale=tiles["x_scales", span][:, cols],
-                            start=(g == 0),
-                            stop=(g == G - 1),
-                        )
+                        layer1_pass(bank[:, t, :], span, lo, width, t, g, g == 0, g == G - 1)
                 tiles["hidden_bank", first + lo] = (bank, width)
 
         def scaled_relu(engine, dst, src, factor):
@@ -237,10 +241,9 @@ def tile_cnn_pa_t_kernel(tc, x_bytes, x_scale, w0, w1, out):
         w1_bank = transpose_weights(w1_sb, 1, 0)
 
 
-        widen("V", 0, 0, 0)
-        widen("S", 0, 0, 1, 0, D // 2)
-        widen("V", 0, 0, 1, D // 2)
-        widen("V", 0, 1, 0)
+        for (g, s), split in zip(((0, 0), (0, 1), (1, 0)), FIRST_SPLITS):
+            widen("V", 0, g, s, 0, split)
+            widen("S", 0, g, s, split)
         widen("S", 0, 1, 1)
         for g in range(G):
             widen("S", 1, g, 1)
@@ -315,19 +318,23 @@ def tile_cnn_pa_t_kernel(tc, x_bytes, x_scale, w0, w1, out):
         interleave([lower[7]])
         first_layer(upper[6])
         first_layer(lower[7])
-        hidden("S", batch[6], lower[6][0])
+        hidden_batch(6)
         finish("S", batch[4])
-        hidden("S", batch[6], upper[6][0])
-        hidden("S", lower[7], lower[7][0])
         interleave([third, fourth])
         second_layer(batch[5])
         finish("S", batch[5])
         first_layer(third)
-        first_layer(fourth)
+        bank = psum.tile([P, 2, fourth[1]], F32, name="hidden_bank", tag="bank")
+        for g in range(G):
+            quantize_x(fourth, g, g + 1)
+            for t in range(2):
+                layer1_pass(bank[:, t, :], fourth, 0, fourth[1], t, g, (g, t) == (0, 0), (g, t) == (G - 1, 1))
+        tiles["hidden_bank", fourth[0]] = (bank, fourth[1])
 
         second_layer(batch[6])
-        second_layer(lower[7])
+        hidden("V", lower[7], lower[7][0])
         hidden("V", upper[7], third[0])
+        second_layer(lower[7])
         hidden("S", upper[7], fourth[0])
         for t in range(2):
             finish_tile("S", batch[6], tiles["out_bank", batch[6][0]][0][:, t, :], t)

@@ -13,7 +13,6 @@ BANK_N = 256
 PASS_WORDS = 256
 
 SHARE = 512
-SHARED_BATCH = 4
 FIRST_SPLITS = (768, 768, 768)
 
 FLOPS = 2 * BS * Q * HID * (2 * CIN) + 2 * BS * R * OUT_DIM * (2 * HID)
@@ -99,7 +98,7 @@ def tile_cnn_pa_t_kernel(tc, x_bytes, x_scale, w0, w1, out):
             else:
                 nc.vector.tensor_scalar(out=dst, in0=values, scalar1=factor, scalar2=None, op0=ALU.mult)
 
-        def interleave(pieces, g0=0, g1=G):
+        def interleave(engine, pieces, g0=0, g1=G):
             n = pieces[0][1]
             b, first = divmod(pieces[0][0], Q)
             grouped = tile_of(("grouped_tile", pieces[0]), wide, [P, len(pieces) * G * n * 4], BF16, "grouped")
@@ -107,7 +106,8 @@ def tile_cnn_pa_t_kernel(tc, x_bytes, x_scale, w0, w1, out):
                 tiles["grouped", piece] = grouped[:, i * G * n * 4 : (i + 1) * G * n * 4]
             words = tiles["widened", b][:].bitcast(F32).rearrange("p (g s q) -> p g s q", g=G, s=2)
             words = words[:, :, :, first : first + len(pieces) * n]
-            nc.vector.tensor_copy(
+            copy = nc.scalar.copy if engine == "S" else nc.vector.tensor_copy
+            copy(
                 out=grouped[:].bitcast(F32).rearrange("p (i g q s) -> p i g q s", g=G, q=n, s=2)[:, :, g0:g1],
                 in_=words.rearrange("p g s (i q) -> p i g q s", q=n)[:, :, g0:g1],
             )
@@ -221,12 +221,12 @@ def tile_cnn_pa_t_kernel(tc, x_bytes, x_scale, w0, w1, out):
         both = slice(0, 2)
         for b, g, s in ((0, 0, 0), (0, 0, 1), (0, 1, 0), (0, 1, 1), (1, 0, 0), (1, 0, 1), (1, 1, 1), (1, 1, 0)):
             load_x(b, g, slice(s, s + 1))
-        for b in (2, 3):
+        for g in range(G):
+            load_x(2, g, both)
+        load_w(w0_sb, w0)
+        for b in (3, 4):
             for g in range(G):
                 load_x(b, g, both)
-        load_w(w0_sb, w0)
-        for g in range(G):
-            load_x(4, g, both)
         load_w(w1_sb, w1)
         for b in range(5, BS):
             load_x(b, both, both)
@@ -238,8 +238,10 @@ def tile_cnn_pa_t_kernel(tc, x_bytes, x_scale, w0, w1, out):
         ident = keep.tile([P, P], F32, name="ident")
         make_identity(nc, ident[:])
         w0_banks = [transpose_weights(w0_sb, G, g) for g in range(G)]
-        w1_bank = transpose_weights(w1_sb, 1, 0)
 
+        def widen_pass(b, g):
+            widen("V", b, g, 0)
+            widen("V", b, g, 1, SHARE if (b, g) == (5, 0) else 0)
 
         for (g, s), split in zip(((0, 0), (0, 1), (1, 0)), FIRST_SPLITS):
             widen("V", 0, g, s, 0, split)
@@ -248,79 +250,62 @@ def tile_cnn_pa_t_kernel(tc, x_bytes, x_scale, w0, w1, out):
         for g in range(G):
             widen("S", 1, g, 1)
         for g in range(G):
-            interleave([batch[0]], g, g + 1)
+            interleave("V", [batch[0]], g, g + 1)
             widen("V", 1, g, 0)
             quantize_x(batch[0], g, g + 1)
 
-        for b in (2, 3):
-            for g in range(G):
-                widen("S", b, g, 1)
-        widen("S", 4, 0, 1)
+        for g in range(G):
+            widen("S", 2, g, 1)
+        widen("S", 3, 0, 1)
         for g in range(G):
             weights_out(w0_banks[g], w0_grouped[:, g * HID * 4 : (g + 1) * HID * 4])
+        w1_bank = transpose_weights(w1_sb, 1, 0)
+        widen("S", 3, 1, 1)
+        widen("S", 4, 0, 1)
         widen("S", 4, 1, 1)
-        widen("S", SHARED_BATCH, 1, 0, 0, SHARE)
         weights_out(w1_bank, w1_grouped[:])
-
-        for b in (1, 2):
-            interleave([batch[b]])
-            for g in range(G):
-                widen("V", b + 1, g, 0)
-            quantize_x(batch[b])
-        quantize_w(w0_grouped, w0_codes, w0_scales)
-        for b in range(3):
-            layer1(batch[b])
-
+        widen("S", 5, 0, 1, 0, SHARE)
+        interleave("V", [batch[1]])
         for g in range(G):
-            widen("S", 5, g, 1)
+            widen("V", 2, g, 0)
+        quantize_x(batch[1])
+        interleave("V", [batch[2]])
+        quantize_w(w0_grouped, w0_codes, w0_scales)
+        for b in range(2):
+            layer1(batch[b])
+        for g in range(G):
+            widen("V", 3, g, 0)
+        first_layer(batch[2])
+        for g in range(G):
+            widen("V", 4, g, 0)
         hidden_batch(0)
         hidden_batch(1)
-        interleave([lower[3], upper[3]])
-        widen("V", 4, 0, 0)
+        interleave("V", [lower[3], upper[3]])
         quantize_w(w1_grouped, w1_codes, w1_scales)
-        widen("V", SHARED_BATCH, 1, 0, SHARE)
-        first_layer(lower[3])
 
-        widen("S", 6, 0, 1)
-        hidden_batch(2)
-        interleave([lower[4], upper[4]])
-        first_layer(upper[3])
-        for g in range(G):
-            widen("V", 5, g, 0)
-            second_layer(batch[g])
-        finish("S", batch[0])
-        first_layer(lower[4])
+        for b in (3, 4, 5):
+            interleave("S", [lower[b + 1], upper[b + 1]])
+            widen_pass(b + 2, 0)
+            first_layer(lower[b])
+            second_layer(batch[b - 3])
+            if b > 3:
+                finish("S", batch[b - 4])
+            hidden_batch(b - 1)
+            widen_pass(b + 2, 1)
+            first_layer(upper[b])
 
-        widen("S", 6, 1, 1)
-        hidden_batch(3)
-        finish("S", batch[1])
-        interleave([lower[5], upper[5]])
-        first_layer(upper[4])
-        widen("V", 6, 0, 0)
-        second_layer(batch[2])
-        hidden_batch(4)
-        for g in range(G):
-            widen("S", 7, g, 1)
         finish("S", batch[2])
-        widen("V", 6, 1, 0)
-        first_layer(lower[5])
-
-        interleave([lower[6], upper[6]])
-        first_layer(upper[5])
-        widen("V", 7, 0, 0)
         second_layer(batch[3])
-        second_layer(batch[4])
+        first_layer(lower[6])
+        interleave("V", [lower[7]])
         hidden_batch(5)
         finish("S", batch[3])
-        widen("V", 7, 1, 0)
-        first_layer(lower[6])
-
-        interleave([lower[7]])
         first_layer(upper[6])
+        second_layer(batch[4])
         first_layer(lower[7])
         hidden_batch(6)
         finish("S", batch[4])
-        interleave([third, fourth])
+        interleave("V", [third, fourth])
         second_layer(batch[5])
         finish("S", batch[5])
         first_layer(third)

@@ -12,8 +12,8 @@ G = 2
 BANK_N = 256
 PASS_WORDS = 256
 
-SHARE = 512
-FIRST_SPLITS = (768, 768, 768)
+SHARE = D // 2
+FIRST_SPLIT = 3 * D // 4
 
 FLOPS = 2 * BS * Q * HID * (2 * CIN) + 2 * BS * R * OUT_DIM * (2 * HID)
 
@@ -98,7 +98,7 @@ def tile_cnn_pa_t_kernel(tc, x_bytes, x_scale, w0, w1, out):
             else:
                 nc.vector.tensor_scalar(out=dst, in0=values, scalar1=factor, scalar2=None, op0=ALU.mult)
 
-        def interleave(engine, pieces, g0=0, g1=G):
+        def interleave(pieces, g0=0, g1=G):
             n = pieces[0][1]
             b, first = divmod(pieces[0][0], Q)
             grouped = tile_of(("grouped_tile", pieces[0]), wide, [P, len(pieces) * G * n * 4], BF16, "grouped")
@@ -106,8 +106,7 @@ def tile_cnn_pa_t_kernel(tc, x_bytes, x_scale, w0, w1, out):
                 tiles["grouped", piece] = grouped[:, i * G * n * 4 : (i + 1) * G * n * 4]
             words = tiles["widened", b][:].bitcast(F32).rearrange("p (g s q) -> p g s q", g=G, s=2)
             words = words[:, :, :, first : first + len(pieces) * n]
-            copy = nc.scalar.copy if engine == "S" else nc.vector.tensor_copy
-            copy(
+            nc.vector.tensor_copy(
                 out=grouped[:].bitcast(F32).rearrange("p (i g q s) -> p i g q s", g=G, q=n, s=2)[:, :, g0:g1],
                 in_=words.rearrange("p g s (i q) -> p i g q s", q=n)[:, :, g0:g1],
             )
@@ -239,18 +238,14 @@ def tile_cnn_pa_t_kernel(tc, x_bytes, x_scale, w0, w1, out):
         make_identity(nc, ident[:])
         w0_banks = [transpose_weights(w0_sb, G, g) for g in range(G)]
 
-        def widen_pass(b, g):
-            widen("V", b, g, 0)
-            widen("V", b, g, 1, SHARE if (b, g) == (5, 0) else 0)
-
-        for (g, s), split in zip(((0, 0), (0, 1), (1, 0)), FIRST_SPLITS):
-            widen("V", 0, g, s, 0, split)
-            widen("S", 0, g, s, split)
+        for g, s in ((0, 0), (0, 1), (1, 0)):
+            widen("V", 0, g, s, 0, FIRST_SPLIT)
+            widen("S", 0, g, s, FIRST_SPLIT)
         widen("S", 0, 1, 1)
         for g in range(G):
             widen("S", 1, g, 1)
         for g in range(G):
-            interleave("V", [batch[0]], g, g + 1)
+            interleave([batch[0]], g, g + 1)
             widen("V", 1, g, 0)
             quantize_x(batch[0], g, g + 1)
 
@@ -261,43 +256,45 @@ def tile_cnn_pa_t_kernel(tc, x_bytes, x_scale, w0, w1, out):
             weights_out(w0_banks[g], w0_grouped[:, g * HID * 4 : (g + 1) * HID * 4])
         w1_bank = transpose_weights(w1_sb, 1, 0)
         widen("S", 3, 1, 1)
-        widen("S", 4, 0, 1)
-        widen("S", 4, 1, 1)
+        for g in range(G):
+            widen("S", 4, g, 1)
         weights_out(w1_bank, w1_grouped[:])
-        widen("S", 5, 0, 1, 0, SHARE)
-        interleave("V", [batch[1]])
+        widen("S", 4, 1, 0, 0, SHARE)
+        interleave([batch[1]])
         for g in range(G):
             widen("V", 2, g, 0)
         quantize_x(batch[1])
-        interleave("V", [batch[2]])
+        interleave([batch[2]])
         quantize_w(w0_grouped, w0_codes, w0_scales)
         for b in range(2):
             layer1(batch[b])
         for g in range(G):
             widen("V", 3, g, 0)
         first_layer(batch[2])
-        for g in range(G):
-            widen("V", 4, g, 0)
         hidden_batch(0)
         hidden_batch(1)
-        interleave("V", [lower[3], upper[3]])
+        interleave([lower[3], upper[3]])
+        widen("V", 4, 0, 0)
         quantize_w(w1_grouped, w1_codes, w1_scales)
+        widen("V", 4, 1, 0, SHARE)
 
         for b in (3, 4, 5):
-            interleave("S", [lower[b + 1], upper[b + 1]])
-            widen_pass(b + 2, 0)
+            for g in range(G):
+                widen("S", b + 2, g, 1)
             first_layer(lower[b])
+            interleave([lower[b + 1], upper[b + 1]])
+            first_layer(upper[b])
             second_layer(batch[b - 3])
             if b > 3:
                 finish("S", batch[b - 4])
             hidden_batch(b - 1)
-            widen_pass(b + 2, 1)
-            first_layer(upper[b])
+            for g in range(G):
+                widen("V", b + 2, g, 0)
 
         finish("S", batch[2])
         second_layer(batch[3])
         first_layer(lower[6])
-        interleave("V", [lower[7]])
+        interleave([lower[7]])
         hidden_batch(5)
         finish("S", batch[3])
         first_layer(upper[6])
@@ -305,7 +302,7 @@ def tile_cnn_pa_t_kernel(tc, x_bytes, x_scale, w0, w1, out):
         first_layer(lower[7])
         hidden_batch(6)
         finish("S", batch[4])
-        interleave("V", [third, fourth])
+        interleave([third, fourth])
         second_layer(batch[5])
         finish("S", batch[5])
         first_layer(third)

@@ -12,7 +12,8 @@ G = 2
 BANK_N = 256
 PASS_WORDS = 256
 
-SHARE = D // 2
+SHARE = D // 4
+SHARED = 4
 FIRST_SPLIT = 3 * D // 4
 
 FLOPS = 2 * BS * Q * HID * (2 * CIN) + 2 * BS * R * OUT_DIM * (2 * HID)
@@ -35,9 +36,10 @@ def tile_cnn_pa_t_kernel(tc, x_bytes, x_scale, w0, w1, out):
 
     with ExitStack() as ctx:
         keep = ctx.enter_context(tc.tile_pool(name="keep", bufs=1))
-        outp = ctx.enter_context(tc.tile_pool(name="outp", bufs=8))
-        wide = ctx.enter_context(tc.tile_pool(name="wide", bufs=5))
-        work = ctx.enter_context(tc.tile_pool(name="work", bufs=5))
+        outp = ctx.enter_context(tc.tile_pool(name="outp", bufs=BS + 3))
+        wide = ctx.enter_context(tc.tile_pool(name="wide", bufs=BS))
+        hid = ctx.enter_context(tc.tile_pool(name="hid", bufs=BS + 1))
+        group = ctx.enter_context(tc.tile_pool(name="group", bufs=3))
         psum = ctx.enter_context(tc.psum_pool(name="psum", bufs=8))
         ctx.enter_context(tc.manual_schedule())
 
@@ -50,11 +52,11 @@ def tile_cnn_pa_t_kernel(tc, x_bytes, x_scale, w0, w1, out):
 
         scale_sb = keep.tile([P, G, 8], F32, name="scale_sb")
         nc.scalar.dma_start(out=scale_sb[:, :, 0:2], in_=x_scale.rearrange("o (g p s) x -> p g (o s x)", g=G, p=P, s=2))
-        x_rows = x_bytes.rearrange("b (g p s) d -> p g s b d", g=G, p=P, s=2)
+        x_rows = x_bytes.rearrange("b (g p s) d -> p (b g) s d", g=G, p=P, s=2)
+        x_sb = keep.tile([P, BS * G, 2, D], U8, name="x_sb", align_bytes=64)
 
-        def load_x(b, passes, slots):
-            x_sb = tile_of(("x", b), keep, [P, G, 2, D], U8, "x_%d" % b)
-            nc.sync.dma_start(out=x_sb[:, passes, slots], in_=x_rows[:, passes, slots, b])
+        def load_x(first, last, slots=slice(0, 2)):
+            nc.sync.dma_start(out=x_sb[:, first:last, slots], in_=x_rows[:, first:last, slots])
 
         w0_sb = keep.tile([P, 2 * 2 * CIN], BF16, name="w0_sb", align_bytes=64)
         w1_sb = keep.tile([P, 2 * 2 * HID], BF16, name="w1_sb", align_bytes=64)
@@ -88,7 +90,7 @@ def tile_cnn_pa_t_kernel(tc, x_bytes, x_scale, w0, w1, out):
             nc.vector.quantize_mx(out=codes[:].bitcast(FP8X4), scales=scales[:], in_=grouped[:])
 
         def widen(engine, b, g, s, first=0, last=D):
-            values = tiles["x", b][:, g, s, first:last].bitcast(FP8)
+            values = x_sb[:, G * b + g, s, first:last].bitcast(FP8)
             widened = tile_of(("widened", b), wide, [P, G * 2 * D], BF16, "widened")
             row = (2 * g + s) * D
             dst = widened[:, row + first : row + last]
@@ -101,7 +103,7 @@ def tile_cnn_pa_t_kernel(tc, x_bytes, x_scale, w0, w1, out):
         def interleave(pieces, g0=0, g1=G):
             n = pieces[0][1]
             b, first = divmod(pieces[0][0], Q)
-            grouped = tile_of(("grouped_tile", pieces[0]), wide, [P, len(pieces) * G * n * 4], BF16, "grouped")
+            grouped = tile_of(("grouped_tile", pieces[0]), group, [P, len(pieces) * G * n * 4], BF16, "grouped")
             for i, piece in enumerate(pieces):
                 tiles["grouped", piece] = grouped[:, i * G * n * 4 : (i + 1) * G * n * 4]
             words = tiles["widened", b][:].bitcast(F32).rearrange("p (g s q) -> p g s q", g=G, s=2)
@@ -113,8 +115,8 @@ def tile_cnn_pa_t_kernel(tc, x_bytes, x_scale, w0, w1, out):
 
         def quantize_x(span, g0=0, g1=G):
             n = span[1]
-            codes = tile_of(("x_codes", span), work, [P, G * n], U32, "x_codes")
-            scales = tile_of(("x_scales", span), work, [P, G * n], U8, "x_scales")
+            codes = tile_of(("x_codes", span), keep, [P, G * n], U32, "x_codes_%d" % span[0])
+            scales = tile_of(("x_scales", span), keep, [P, G * n], U8, "x_scales_%d" % span[0])
             nc.vector.quantize_mx(
                 out=codes[:, g0 * n : g1 * n].bitcast(FP8X4),
                 scales=scales[:, g0 * n : g1 * n],
@@ -152,16 +154,19 @@ def tile_cnn_pa_t_kernel(tc, x_bytes, x_scale, w0, w1, out):
 
         def hidden(engine, h_span, first):
             bank, width = tiles["hidden_bank", first]
-            h = tile_of(("h", h_span), work, [P, 2 * h_span[1]], BF16, "h")
+            h = tile_of(("h", h_span), hid, [P, 2 * h_span[1]], BF16, "h")
             lo = first - h_span[0]
             dst = h[:, 2 * lo : 2 * (lo + width)].rearrange("p (r s k) -> p r s k", s=2, k=2)
             scaled_relu(engine, dst, bank[:].rearrange("p s (r k) -> p r s k", k=2), SCALE0)
 
-        def quantize_h(h_span):
+        def quantize_h(h_span, part=0, parts=1):
             n = h_span[1] // 2
-            codes = tile_of(("h_codes", h_span), work, [P, n], U32, "h_codes")
-            scales = tile_of(("h_scales", h_span), work, [P, n], U8, "h_scales")
-            nc.vector.quantize_mx(out=codes[:].bitcast(FP8X4), scales=scales[:], in_=tiles["h", h_span][:])
+            lo, hi = part * n // parts, (part + 1) * n // parts
+            codes = tile_of(("h_codes", h_span), hid, [P, n], U32, "h_codes")
+            scales = tile_of(("h_scales", h_span), hid, [P, n], U8, "h_scales")
+            nc.vector.quantize_mx(
+                out=codes[:, lo:hi].bitcast(FP8X4), scales=scales[:, lo:hi], in_=tiles["h", h_span][:, 4 * lo : 4 * hi]
+            )
 
         def layer2_pass(dst, h_span, lo, width, t):
             w_cols = slice(t * P, (t + 1) * P)
@@ -217,18 +222,16 @@ def tile_cnn_pa_t_kernel(tc, x_bytes, x_scale, w0, w1, out):
             quantize_h(h_span)
             layer2(h_span)
 
-        both = slice(0, 2)
-        for b, g, s in ((0, 0, 0), (0, 0, 1), (0, 1, 0), (0, 1, 1), (1, 0, 0), (1, 0, 1), (1, 1, 1), (1, 1, 0)):
-            load_x(b, g, slice(s, s + 1))
+        for bg in range(2 * G):
+            for s in range(2):
+                load_x(bg, bg + 1, slice(s, s + 1))
         for g in range(G):
-            load_x(2, g, both)
+            load_x(2 * G + g, 2 * G + g + 1)
         load_w(w0_sb, w0)
-        for b in (3, 4):
-            for g in range(G):
-                load_x(b, g, both)
+        load_x(3 * G, 4 * G)
         load_w(w1_sb, w1)
-        for b in range(5, BS):
-            load_x(b, both, both)
+        load_x(4 * G, 6 * G)
+        load_x(6 * G, 8 * G)
 
         warm = keep.tile([P, 1], F32, name="warm")
         nc.vector.memset(warm[:], 0.0)
@@ -238,72 +241,71 @@ def tile_cnn_pa_t_kernel(tc, x_bytes, x_scale, w0, w1, out):
         make_identity(nc, ident[:])
         w0_banks = [transpose_weights(w0_sb, G, g) for g in range(G)]
 
+        def widen_slot1(b, first=0, last=D):
+            for g in range(G):
+                widen("S", b, g, 1, first, last)
+
+        def step(b, pieces, previous):
+            widen("V", b + 1, 0, 0)
+            for span in previous:
+                first_layer(span)
+            widen("V", b + 1, 1, 0, SHARE if b + 1 == SHARED else 0)
+            interleave(pieces)
+
         for g, s in ((0, 0), (0, 1), (1, 0)):
             widen("V", 0, g, s, 0, FIRST_SPLIT)
             widen("S", 0, g, s, FIRST_SPLIT)
         widen("S", 0, 1, 1)
-        for g in range(G):
-            widen("S", 1, g, 1)
-        for g in range(G):
-            interleave([batch[0]], g, g + 1)
-            widen("V", 1, g, 0)
-            quantize_x(batch[0], g, g + 1)
+        widen_slot1(1)
+        interleave([batch[0]], 0, 1)
+        widen("V", 1, 0, 0)
+        quantize_x(batch[0], 0, 1)
+        widen("V", 1, 1, 0)
+        interleave([batch[0]], 1, 2)
+        widen("V", 2, 0, 0)
+        quantize_x(batch[0], 1, 2)
+        widen("V", 2, 1, 0)
+        interleave([batch[1]])
 
-        for g in range(G):
-            widen("S", 2, g, 1)
-        widen("S", 3, 0, 1)
+        widen_slot1(2)
         for g in range(G):
             weights_out(w0_banks[g], w0_grouped[:, g * HID * 4 : (g + 1) * HID * 4])
         w1_bank = transpose_weights(w1_sb, 1, 0)
-        widen("S", 3, 1, 1)
-        for g in range(G):
-            widen("S", 4, g, 1)
+        widen_slot1(3)
         weights_out(w1_bank, w1_grouped[:])
-        widen("S", 4, 1, 0, 0, SHARE)
-        interleave([batch[1]])
-        for g in range(G):
-            widen("V", 2, g, 0)
+        widen("S", SHARED, 1, 0, 0, SHARE)
+        widen("V", 3, 0, 0)
         quantize_x(batch[1])
-        interleave([batch[2]])
         quantize_w(w0_grouped, w0_codes, w0_scales)
         for b in range(2):
             layer1(batch[b])
-        for g in range(G):
-            widen("V", 3, g, 0)
-        first_layer(batch[2])
-        hidden_batch(0)
-        hidden_batch(1)
-        interleave([lower[3], upper[3]])
-        widen("V", 4, 0, 0)
+        widen("V", 3, 1, 0)
+        interleave([batch[2]])
+        for b in range(2):
+            widen("S", 4, b, 1)
+            hidden_batch(b)
+
+        step(3, [batch[3]], [batch[2]])
         quantize_w(w1_grouped, w1_codes, w1_scales)
-        widen("V", 4, 1, 0, SHARE)
-
-        for b in (3, 4, 5):
-            for g in range(G):
-                widen("S", b + 2, g, 1)
-            first_layer(lower[b])
-            interleave([lower[b + 1], upper[b + 1]])
-            first_layer(upper[b])
+        second_layer(batch[0])
+        for b in (4, 5, 6):
+            widen_slot1(b + 1)
+            hidden_batch(b - 2)
+            finish("S", batch[b - 4])
+            step(b, [batch[b]] if b < 5 else [lower[b], upper[b]], [batch[b - 1]] if b < 6 else [lower[b - 1], upper[b - 1]])
             second_layer(batch[b - 3])
-            if b > 3:
-                finish("S", batch[b - 4])
-            hidden_batch(b - 1)
-            for g in range(G):
-                widen("V", b + 2, g, 0)
 
-        finish("S", batch[2])
-        second_layer(batch[3])
+        hidden_batch(5)
         first_layer(lower[6])
         interleave([lower[7]])
-        hidden_batch(5)
-        finish("S", batch[3])
         first_layer(upper[6])
         second_layer(batch[4])
+        finish("S", batch[3])
         first_layer(lower[7])
         hidden_batch(6)
-        finish("S", batch[4])
         interleave([third, fourth])
         second_layer(batch[5])
+        finish("S", batch[4])
         finish("S", batch[5])
         first_layer(third)
         bank = psum.tile([P, 2, fourth[1]], F32, name="hidden_bank", tag="bank")
@@ -320,7 +322,8 @@ def tile_cnn_pa_t_kernel(tc, x_bytes, x_scale, w0, w1, out):
         hidden("S", upper[7], fourth[0])
         for t in range(2):
             finish_tile("S", batch[6], tiles["out_bank", batch[6][0]][0][:, t, :], t)
-        quantize_h(upper[7])
+        for part in range(2):
+            quantize_h(upper[7], part, 2)
         finish("V", lower[7])
         for t, engine in enumerate("VS"):
             bank = psum.tile([P, upper[7][1] // 2], F32, name="last_bank", tag="bank")

@@ -12,8 +12,7 @@ G = 2
 BANK_N = 256
 PASS_WORDS = 256
 
-SHARE = D // 4
-SHARED = 4
+SHARE = D // 2
 FIRST_SPLIT = 3 * D // 4
 
 FLOPS = 2 * BS * Q * HID * (2 * CIN) + 2 * BS * R * OUT_DIM * (2 * HID)
@@ -36,10 +35,9 @@ def tile_cnn_pa_t_kernel(tc, x_bytes, x_scale, w0, w1, out):
 
     with ExitStack() as ctx:
         keep = ctx.enter_context(tc.tile_pool(name="keep", bufs=1))
-        outp = ctx.enter_context(tc.tile_pool(name="outp", bufs=BS + 3))
-        wide = ctx.enter_context(tc.tile_pool(name="wide", bufs=BS))
+        outp = ctx.enter_context(tc.tile_pool(name="outp", bufs=BS))
         hid = ctx.enter_context(tc.tile_pool(name="hid", bufs=BS + 1))
-        group = ctx.enter_context(tc.tile_pool(name="group", bufs=3))
+        mixed = ctx.enter_context(tc.tile_pool(name="mixed", bufs=3))
         psum = ctx.enter_context(tc.psum_pool(name="psum", bufs=8))
         ctx.enter_context(tc.manual_schedule())
 
@@ -52,11 +50,14 @@ def tile_cnn_pa_t_kernel(tc, x_bytes, x_scale, w0, w1, out):
 
         scale_sb = keep.tile([P, G, 8], F32, name="scale_sb")
         nc.scalar.dma_start(out=scale_sb[:, :, 0:2], in_=x_scale.rearrange("o (g p s) x -> p g (o s x)", g=G, p=P, s=2))
-        x_rows = x_bytes.rearrange("b (g p s) d -> p (b g) s d", g=G, p=P, s=2)
-        x_sb = keep.tile([P, BS * G, 2, D], U8, name="x_sb", align_bytes=64)
+        groups = [(0, 1), (1, 1), (2, 2), (4, 2), (6, 2)]
+        group_of = {b: group for group in groups for b in range(group[0], group[0] + group[1])}
+        x_rows = x_bytes.rearrange("b (g p s) d -> p g s b d", g=G, p=P, s=2)
 
-        def load_x(first, last, slots=slice(0, 2)):
-            nc.sync.dma_start(out=x_sb[:, first:last, slots], in_=x_rows[:, first:last, slots])
+        def load_x(group, g, slots):
+            first, n = group
+            x_sb = tile_of(("x", group), keep, [P, G, 2, n, D], U8, "x_%d" % first)
+            nc.sync.dma_start(out=x_sb[:, g, slots], in_=x_rows[:, g, slots, first : first + n])
 
         w0_sb = keep.tile([P, 2 * 2 * CIN], BF16, name="w0_sb", align_bytes=64)
         w1_sb = keep.tile([P, 2 * 2 * HID], BF16, name="w1_sb", align_bytes=64)
@@ -89,10 +90,12 @@ def tile_cnn_pa_t_kernel(tc, x_bytes, x_scale, w0, w1, out):
         def quantize_w(grouped, codes, scales):
             nc.vector.quantize_mx(out=codes[:].bitcast(FP8X4), scales=scales[:], in_=grouped[:])
 
-        def widen(engine, b, g, s, first=0, last=D):
-            values = x_sb[:, G * b + g, s, first:last].bitcast(FP8)
-            widened = tile_of(("widened", b), wide, [P, G * 2 * D], BF16, "widened")
-            row = (2 * g + s) * D
+        def widen(engine, group, g, s, first=0, last=None):
+            width = group[1] * D
+            last = width if last is None else last
+            values = tiles["x", group][:, g, s].rearrange("p b d -> p (b d)")[:, first:last].bitcast(FP8)
+            widened = tile_of(("widened", group), keep, [P, G * 2 * width], BF16, "widened_%d" % group[0])
+            row = (2 * g + s) * width
             dst = widened[:, row + first : row + last]
             factor = scale_sb[:, g, s : s + 1]
             if engine == "S":
@@ -102,11 +105,12 @@ def tile_cnn_pa_t_kernel(tc, x_bytes, x_scale, w0, w1, out):
 
         def interleave(pieces, g0=0, g1=G):
             n = pieces[0][1]
-            b, first = divmod(pieces[0][0], Q)
-            grouped = tile_of(("grouped_tile", pieces[0]), group, [P, len(pieces) * G * n * 4], BF16, "grouped")
+            group = group_of[pieces[0][0] // Q]
+            first = pieces[0][0] - group[0] * Q
+            grouped = tile_of(("grouped_tile", pieces[0]), mixed, [P, len(pieces) * G * n * 4], BF16, "grouped")
             for i, piece in enumerate(pieces):
                 tiles["grouped", piece] = grouped[:, i * G * n * 4 : (i + 1) * G * n * 4]
-            words = tiles["widened", b][:].bitcast(F32).rearrange("p (g s q) -> p g s q", g=G, s=2)
+            words = tiles["widened", group][:].bitcast(F32).rearrange("p (g s q) -> p g s q", g=G, s=2)
             words = words[:, :, :, first : first + len(pieces) * n]
             nc.vector.tensor_copy(
                 out=grouped[:].bitcast(F32).rearrange("p (i g q s) -> p i g q s", g=G, q=n, s=2)[:, :, g0:g1],
@@ -159,14 +163,11 @@ def tile_cnn_pa_t_kernel(tc, x_bytes, x_scale, w0, w1, out):
             dst = h[:, 2 * lo : 2 * (lo + width)].rearrange("p (r s k) -> p r s k", s=2, k=2)
             scaled_relu(engine, dst, bank[:].rearrange("p s (r k) -> p r s k", k=2), SCALE0)
 
-        def quantize_h(h_span, part=0, parts=1):
+        def quantize_h(h_span):
             n = h_span[1] // 2
-            lo, hi = part * n // parts, (part + 1) * n // parts
             codes = tile_of(("h_codes", h_span), hid, [P, n], U32, "h_codes")
             scales = tile_of(("h_scales", h_span), hid, [P, n], U8, "h_scales")
-            nc.vector.quantize_mx(
-                out=codes[:, lo:hi].bitcast(FP8X4), scales=scales[:, lo:hi], in_=tiles["h", h_span][:, 4 * lo : 4 * hi]
-            )
+            nc.vector.quantize_mx(out=codes[:].bitcast(FP8X4), scales=scales[:], in_=tiles["h", h_span][:])
 
         def layer2_pass(dst, h_span, lo, width, t):
             w_cols = slice(t * P, (t + 1) * P)
@@ -222,16 +223,13 @@ def tile_cnn_pa_t_kernel(tc, x_bytes, x_scale, w0, w1, out):
             quantize_h(h_span)
             layer2(h_span)
 
-        for bg in range(2 * G):
-            for s in range(2):
-                load_x(bg, bg + 1, slice(s, s + 1))
-        for g in range(G):
-            load_x(2 * G + g, 2 * G + g + 1)
-        load_w(w0_sb, w0)
-        load_x(3 * G, 4 * G)
-        load_w(w1_sb, w1)
-        load_x(4 * G, 6 * G)
-        load_x(6 * G, 8 * G)
+        weights_after = {groups[2]: (w0_sb, w0), groups[3]: (w1_sb, w1)}
+        for group in groups:
+            for g in range(G):
+                for slots in [slice(0, 2)] if group == groups[1] else [slice(0, 1), slice(1, 2)]:
+                    load_x(group, g, slots)
+            if group in weights_after:
+                load_w(*weights_after[group])
 
         warm = keep.tile([P, 1], F32, name="warm")
         nc.vector.memset(warm[:], 0.0)
@@ -241,59 +239,64 @@ def tile_cnn_pa_t_kernel(tc, x_bytes, x_scale, w0, w1, out):
         make_identity(nc, ident[:])
         w0_banks = [transpose_weights(w0_sb, G, g) for g in range(G)]
 
-        def widen_slot1(b, first=0, last=D):
-            for g in range(G):
-                widen("S", b, g, 1, first, last)
-
-        def step(b, pieces, previous):
-            widen("V", b + 1, 0, 0)
-            for span in previous:
-                first_layer(span)
-            widen("V", b + 1, 1, 0, SHARE if b + 1 == SHARED else 0)
-            interleave(pieces)
-
         for g, s in ((0, 0), (0, 1), (1, 0)):
-            widen("V", 0, g, s, 0, FIRST_SPLIT)
-            widen("S", 0, g, s, FIRST_SPLIT)
-        widen("S", 0, 1, 1)
-        widen_slot1(1)
+            widen("V", groups[0], g, s, 0, FIRST_SPLIT)
+            widen("S", groups[0], g, s, FIRST_SPLIT)
+        widen("S", groups[0], 1, 1)
+        for g in range(G):
+            widen("S", groups[1], g, 1)
         interleave([batch[0]], 0, 1)
-        widen("V", 1, 0, 0)
+        widen("V", groups[1], 0, 0)
         quantize_x(batch[0], 0, 1)
-        widen("V", 1, 1, 0)
+        widen("V", groups[1], 1, 0)
         interleave([batch[0]], 1, 2)
-        widen("V", 2, 0, 0)
+        widen("V", groups[2], 0, 0)
         quantize_x(batch[0], 1, 2)
-        widen("V", 2, 1, 0)
         interleave([batch[1]])
 
-        widen_slot1(2)
+        for g in range(G):
+            widen("S", groups[2], g, 1)
         for g in range(G):
             weights_out(w0_banks[g], w0_grouped[:, g * HID * 4 : (g + 1) * HID * 4])
         w1_bank = transpose_weights(w1_sb, 1, 0)
-        widen_slot1(3)
+        for g in range(G):
+            widen("S", groups[3], g, 1)
         weights_out(w1_bank, w1_grouped[:])
-        widen("S", SHARED, 1, 0, 0, SHARE)
-        widen("V", 3, 0, 0)
+        widen("S", groups[3], 1, 0, 0, SHARE)
+        widen("V", groups[2], 1, 0)
         quantize_x(batch[1])
+        widen("V", groups[3], 0, 0)
+        interleave([batch[2]])
         quantize_w(w0_grouped, w0_codes, w0_scales)
         for b in range(2):
             layer1(batch[b])
-        widen("V", 3, 1, 0)
-        interleave([batch[2]])
-        for b in range(2):
-            widen("S", 4, b, 1)
             hidden_batch(b)
-
-        step(3, [batch[3]], [batch[2]])
+        first_layer(batch[2])
+        interleave([batch[3]])
+        widen("V", groups[3], 1, 0, SHARE)
+        first_layer(batch[3])
+        widen("S", groups[4], 0, 1)
+        hidden_batch(2)
+        widen("S", groups[4], 1, 1)
+        interleave([lower[4], upper[4]])
         quantize_w(w1_grouped, w1_codes, w1_scales)
         second_layer(batch[0])
-        for b in (4, 5, 6):
-            widen_slot1(b + 1)
-            hidden_batch(b - 2)
-            finish("S", batch[b - 4])
-            step(b, [batch[b]] if b < 5 else [lower[b], upper[b]], [batch[b - 1]] if b < 6 else [lower[b - 1], upper[b - 1]])
-            second_layer(batch[b - 3])
+        first_layer(lower[4])
+        widen("V", groups[4], 0, 0)
+        first_layer(upper[4])
+        finish("S", batch[0])
+        interleave([lower[5], upper[5]])
+        second_layer(batch[1])
+        widen("V", groups[4], 1, 0)
+        hidden_batch(3)
+        finish("S", batch[1])
+        first_layer(lower[5])
+        second_layer(batch[2])
+        interleave([lower[6], upper[6]])
+        first_layer(upper[5])
+        hidden_batch(4)
+        finish("S", batch[2])
+        second_layer(batch[3])
 
         hidden_batch(5)
         first_layer(lower[6])
@@ -322,8 +325,7 @@ def tile_cnn_pa_t_kernel(tc, x_bytes, x_scale, w0, w1, out):
         hidden("S", upper[7], fourth[0])
         for t in range(2):
             finish_tile("S", batch[6], tiles["out_bank", batch[6][0]][0][:, t, :], t)
-        for part in range(2):
-            quantize_h(upper[7], part, 2)
+        quantize_h(upper[7])
         finish("V", lower[7])
         for t, engine in enumerate("VS"):
             bank = psum.tile([P, upper[7][1] // 2], F32, name="last_bank", tag="bank")

@@ -54,10 +54,10 @@ def tile_cnn_pa_t_kernel(tc, x_bytes, x_scale, w0, w1, out):
         group_of = {b: group for group in groups for b in range(group[0], group[0] + group[1])}
         x_rows = x_bytes.rearrange("b (g p s) d -> p g s b d", g=G, p=P, s=2)
 
-        def load_x(group, g, slots):
-            first, n = group
-            x_sb = tile_of(("x", group), keep, [P, G, 2, n, D], U8, "x_%d" % first)
-            nc.sync.dma_start(out=x_sb[:, g, slots], in_=x_rows[:, g, slots, first : first + n])
+        def load_x(b, g, slots):
+            first, n = group_of[b]
+            x_sb = tile_of(("x", group_of[b]), keep, [P, G, 2, n, D], U8, "x_%d" % first)
+            nc.sync.dma_start(out=x_sb[:, g, slots, b - first], in_=x_rows[:, g, slots, b])
 
         w0_sb = keep.tile([P, 2 * 2 * CIN], BF16, name="w0_sb", align_bytes=64)
         w1_sb = keep.tile([P, 2 * 2 * HID], BF16, name="w1_sb", align_bytes=64)
@@ -226,8 +226,9 @@ def tile_cnn_pa_t_kernel(tc, x_bytes, x_scale, w0, w1, out):
         weights_after = {groups[2]: (w0_sb, w0), groups[3]: (w1_sb, w1)}
         for group in groups:
             for g in range(G):
-                for slots in [slice(0, 2)] if group == groups[1] else [slice(0, 1), slice(1, 2)]:
-                    load_x(group, g, slots)
+                for b in range(group[0], group[0] + group[1]):
+                    for slots in [slice(0, 1), slice(1, 2)] if b == 0 else [slice(0, 2)]:
+                        load_x(b, g, slots)
             if group in weights_after:
                 load_w(*weights_after[group])
 

@@ -35,7 +35,7 @@ def tile_cnn_pa_t_kernel(tc, x_bytes, x_scale, w0, w1, out):
 
     with ExitStack() as ctx:
         keep = ctx.enter_context(tc.tile_pool(name="keep", bufs=1))
-        outp = ctx.enter_context(tc.tile_pool(name="outp", bufs=BS))
+        outp = ctx.enter_context(tc.tile_pool(name="outp", bufs=BS // 2))
         hid = ctx.enter_context(tc.tile_pool(name="hid", bufs=BS + 1))
         mixed = ctx.enter_context(tc.tile_pool(name="mixed", bufs=3))
         psum = ctx.enter_context(tc.psum_pool(name="psum", bufs=8))
@@ -190,21 +190,21 @@ def tile_cnn_pa_t_kernel(tc, x_bytes, x_scale, w0, w1, out):
                     layer2_pass(bank[:, t, :], h_span, lo, width, t)
                 tiles["out_bank", h_span[0] + 2 * lo] = (bank, width)
 
-        def out_rows(first, width):
-            b, lo = divmod(first // 2, R)
-            return out[b].rearrange("(m t) r -> m t r", t=2)[:, :, lo : lo + width]
+        def out_rows(span):
+            b, lo = divmod(span[0] // 2, R)
+            return out[b].rearrange("(m t) r -> m t r", t=2)[:, :, lo : lo + span[1] // 2]
+
+        def out_tile(span):
+            b, lo = divmod(span[0] // 2, R)
+            return tile_of(("out", b), outp, [P, 2, R], F32, "o_sb")[:, :, lo : lo + span[1] // 2]
 
         def finish(engine, span):
-            bank, width = tiles["out_bank", span[0]]
-            o_sb = outp.tile([P, 2, width], F32, name="o_sb", tag="o_sb")
-            scaled_relu(engine, o_sb[:], bank[:], SCALE1)
-            nc.sync.dma_start(out=out_rows(span[0], width), in_=o_sb[:])
+            scaled_relu(engine, out_tile(span), tiles["out_bank", span[0]][0][:], SCALE1)
+            nc.sync.dma_start(out=out_rows(span), in_=out_tile(span))
 
         def finish_tile(engine, span, src, t):
-            width = span[1] // 2
-            o_sb = outp.tile([P, width], F32, name="o_sb", tag="o_sb")
-            scaled_relu(engine, o_sb[:], src, SCALE1)
-            nc.sync.dma_start(out=out_rows(span[0], width)[:, t], in_=o_sb[:])
+            scaled_relu(engine, out_tile(span)[:, t], src, SCALE1)
+            nc.sync.dma_start(out=out_rows(span)[:, t], in_=out_tile(span)[:, t])
 
         batch = [(b * Q, Q) for b in range(BS)]
         lower = [(b * Q, BANK_N) for b in range(BS)]

@@ -36,7 +36,7 @@ def tile_cnn_pa_t_kernel(tc, x_bytes, x_scale, w0, w1, out):
     with ExitStack() as ctx:
         keep = ctx.enter_context(tc.tile_pool(name="keep", bufs=1))
         outp = ctx.enter_context(tc.tile_pool(name="outp", bufs=BS // 2))
-        hid = ctx.enter_context(tc.tile_pool(name="hid", bufs=BS + 1))
+        work = ctx.enter_context(tc.tile_pool(name="work", bufs=5))
         mixed = ctx.enter_context(tc.tile_pool(name="mixed", bufs=3))
         psum = ctx.enter_context(tc.psum_pool(name="psum", bufs=8))
         ctx.enter_context(tc.manual_schedule())
@@ -119,8 +119,8 @@ def tile_cnn_pa_t_kernel(tc, x_bytes, x_scale, w0, w1, out):
 
         def quantize_x(span, g0=0, g1=G):
             n = span[1]
-            codes = tile_of(("x_codes", span), keep, [P, G * n], U32, "x_codes_%d" % span[0])
-            scales = tile_of(("x_scales", span), keep, [P, G * n], U8, "x_scales_%d" % span[0])
+            codes = tile_of(("x_codes", span), work, [P, G * n], U32, "x_codes")
+            scales = tile_of(("x_scales", span), work, [P, G * n], U8, "x_scales")
             nc.vector.quantize_mx(
                 out=codes[:, g0 * n : g1 * n].bitcast(FP8X4),
                 scales=scales[:, g0 * n : g1 * n],
@@ -158,15 +158,15 @@ def tile_cnn_pa_t_kernel(tc, x_bytes, x_scale, w0, w1, out):
 
         def hidden(engine, h_span, first):
             bank, width = tiles["hidden_bank", first]
-            h = tile_of(("h", h_span), hid, [P, 2 * h_span[1]], BF16, "h")
+            h = tile_of(("h", h_span), work, [P, 2 * h_span[1]], BF16, "h")
             lo = first - h_span[0]
             dst = h[:, 2 * lo : 2 * (lo + width)].rearrange("p (r s k) -> p r s k", s=2, k=2)
             scaled_relu(engine, dst, bank[:].rearrange("p s (r k) -> p r s k", k=2), SCALE0)
 
         def quantize_h(h_span):
             n = h_span[1] // 2
-            codes = tile_of(("h_codes", h_span), hid, [P, n], U32, "h_codes")
-            scales = tile_of(("h_scales", h_span), hid, [P, n], U8, "h_scales")
+            codes = tile_of(("h_codes", h_span), work, [P, n], U32, "h_codes")
+            scales = tile_of(("h_scales", h_span), work, [P, n], U8, "h_scales")
             nc.vector.quantize_mx(out=codes[:].bitcast(FP8X4), scales=scales[:], in_=tiles["h", h_span][:])
 
         def layer2_pass(dst, h_span, lo, width, t):
@@ -249,10 +249,10 @@ def tile_cnn_pa_t_kernel(tc, x_bytes, x_scale, w0, w1, out):
         interleave([batch[0]], 0, 1)
         widen("V", groups[1], 0, 0)
         quantize_x(batch[0], 0, 1)
-        widen("V", groups[1], 1, 0)
         interleave([batch[0]], 1, 2)
-        widen("V", groups[2], 0, 0)
+        widen("V", groups[1], 1, 0)
         quantize_x(batch[0], 1, 2)
+        widen("V", groups[2], 0, 0)
         interleave([batch[1]])
 
         for g in range(G):

import math
from contextlib import ExitStack

import concourse.mybir as mybir
from concourse.masks import make_identity

BS, CIN, HID, D, OUT_DIM = 8, 512, 256, 1024, 256
P = 128
Q = D // 2
R = Q // 2
G = 2
BANK_N = 256
PASS_WORDS = 256

SHARE = D // 2
FIRST_SPLIT = 3 * D // 4

FLOPS = 2 * BS * Q * HID * (2 * CIN) + 2 * BS * R * OUT_DIM * (2 * HID)

F32 = mybir.dt.float32
BF16 = mybir.dt.bfloat16
U32 = mybir.dt.uint32
U8 = mybir.dt.uint8
FP8 = mybir.dt.float8_e4m3fn
FP8X4 = mybir.dt.float8_e4m3fn_x4
ACT = mybir.ActivationFunctionType
ALU = mybir.AluOpType

SCALE0 = 1.0 / math.sqrt(CIN)
SCALE1 = 1.0 / math.sqrt(HID)


def tile_cnn_pa_t_kernel(tc, x_bytes, x_scale, w0, w1, out):
    nc = tc.nc

    with ExitStack() as ctx:
        keep = ctx.enter_context(tc.tile_pool(name="keep", bufs=1))
        outp = ctx.enter_context(tc.tile_pool(name="outp", bufs=BS // 2))
        work = ctx.enter_context(tc.tile_pool(name="work", bufs=5))
        mixed = ctx.enter_context(tc.tile_pool(name="mixed", bufs=3))
        psum = ctx.enter_context(tc.psum_pool(name="psum", bufs=8))
        ctx.enter_context(tc.manual_schedule())

        tiles = {}

        def tile_of(key, pool, shape, dtype, name):
            if key not in tiles:
                tiles[key] = pool.tile(shape, dtype, name=name, align_bytes=64)
            return tiles[key]

        scale_sb = keep.tile([P, G, 8], F32, name="scale_sb")
        nc.scalar.dma_start(out=scale_sb[:, :, 0:2], in_=x_scale.rearrange("o (g p s) x -> p g (o s x)", g=G, p=P, s=2))
        groups = [(0, 1), (1, 1), (2, 2), (4, 2), (6, 2)]
        group_of = {b: group for group in groups for b in range(group[0], group[0] + group[1])}
        x_rows = x_bytes.rearrange("b (g p s) d -> p g s b d", g=G, p=P, s=2)

        def load_x(b, g, slots):
            first, n = group_of[b]
            x_sb = tile_of(("x", group_of[b]), keep, [P, G, 2, n, D], U8, "x_%d" % first)
            nc.sync.dma_start(out=x_sb[:, g, slots, b - first], in_=x_rows[:, g, slots, b])

        w0_sb = keep.tile([P, 2 * 2 * CIN], BF16, name="w0_sb", align_bytes=64)
        w1_sb = keep.tile([P, 2 * 2 * HID], BF16, name="w1_sb", align_bytes=64)

        def load_w(w_sb, w):
            nc.sync.dma_start(out=w_sb[:], in_=w.rearrange("(m t) c k -> m (t c k)", t=2))

        w0_codes = keep.tile([P, G * HID], U32, name="w0_codes", align_bytes=64)
        w0_scales = keep.tile([P, G * HID], U8, name="w0_scales", align_bytes=64)
        w0_grouped = keep.tile([P, G * HID * 4], BF16, name="w0_grouped", align_bytes=64)
        w1_codes = keep.tile([P, OUT_DIM], U32, name="w1_codes", align_bytes=64)
        w1_scales = keep.tile([P, OUT_DIM], U8, name="w1_scales", align_bytes=64)
        w1_grouped = keep.tile([P, OUT_DIM * 4], BF16, name="w1_grouped", align_bytes=64)

        def transpose_weights(w_sb, passes, g):
            words = w_sb[:].bitcast(F32)
            bank = psum.tile([P, 2, 2, P], F32, name="weight_bank", tag="bank")
            for t in range(2):
                for s in range(2):
                    lo = (passes * t + g) * PASS_WORDS
                    nc.tensor.transpose(bank[:, t, s, :], words[:, lo + s : lo + PASS_WORDS : 2], ident[:])
            return bank

        def weights_out(bank, dst):
            nc.scalar.copy(
                out=dst.bitcast(F32).rearrange("p (t m s) -> p t m s", t=2, s=2),
                in_=bank[:].rearrange("p t s m -> p t m s"),
            )

        def quantize_w(grouped, codes, scales):
            nc.vector.quantize_mx(out=codes[:].bitcast(FP8X4), scales=scales[:], in_=grouped[:])

        def widen(engine, group, g, s, first=0, last=None):
            width = group[1] * D
            last = width if last is None else last
            values = tiles["x", group][:, g, s].rearrange("p b d -> p (b d)")[:, first:last].bitcast(FP8)
            widened = tile_of(("widened", group), keep, [P, G * 2 * width], BF16, "widened_%d" % group[0])
            row = (2 * g + s) * width
            dst = widened[:, row + first : row + last]
            factor = scale_sb[:, g, s : s + 1]
            if engine == "S":
                nc.scalar.activation(out=dst, in_=values, func=ACT.Copy, scale=factor)
            else:
                nc.vector.tensor_scalar(out=dst, in0=values, scalar1=factor, scalar2=None, op0=ALU.mult)

        def interleave(pieces, g0=0, g1=G):
            n = pieces[0][1]
            group = group_of[pieces[0][0] // Q]
            first = pieces[0][0] - group[0] * Q
            grouped = tile_of(("grouped_tile", pieces[0]), mixed, [P, len(pieces) * G * n * 4], BF16, "grouped")
            for i, piece in enumerate(pieces):
                tiles["grouped", piece] = grouped[:, i * G * n * 4 : (i + 1) * G * n * 4]
            words = tiles["widened", group][:].bitcast(F32).rearrange("p (g s q) -> p g s q", g=G, s=2)
            words = words[:, :, :, first : first + len(pieces) * n]
            nc.vector.tensor_copy(
                out=grouped[:].bitcast(F32).rearrange("p (i g q s) -> p i g q s", g=G, q=n, s=2)[:, :, g0:g1],
                in_=words.rearrange("p g s (i q) -> p i g q s", q=n)[:, :, g0:g1],
            )

        def quantize_x(span, g0=0, g1=G):
            n = span[1]
            codes = tile_of(("x_codes", span), work, [P, G * n], U32, "x_codes")
            scales = tile_of(("x_scales", span), work, [P, G * n], U8, "x_scales")
            nc.vector.quantize_mx(
                out=codes[:, g0 * n : g1 * n].bitcast(FP8X4),
                scales=scales[:, g0 * n : g1 * n],
                in_=tiles["grouped", span][:, 4 * g0 * n : 4 * g1 * n],
            )

        def layer1_pass(dst, span, lo, width, t, g, start, stop):
            cols = slice(g * span[1] + lo, g * span[1] + lo + width)
            w_cols = slice(g * HID + t * P, g * HID + (t + 1) * P)
            nc.tensor.matmul_mx(
                out=dst,
                lhsT=w0_codes[:, w_cols].bitcast(FP8X4),
                lhsT_scale=w0_scales[:, w_cols],
                rhs=tiles["x_codes", span][:, cols].bitcast(FP8X4),
                rhs_scale=tiles["x_scales", span][:, cols],
                start=start,
                stop=stop,
            )

        def layer1(span):
            first, n = span
            width = min(n, BANK_N)
            for lo in range(0, n, width):
                bank = psum.tile([P, 2, width], F32, name="hidden_bank", tag="bank")
                for t in range(2):
                    for g in range(G):
                        layer1_pass(bank[:, t, :], span, lo, width, t, g, g == 0, g == G - 1)
                tiles["hidden_bank", first + lo] = (bank, width)

        def scaled_relu(engine, dst, src, factor):
            if engine == "S":
                nc.scalar.activation(out=dst, in_=src, func=ACT.Relu, scale=factor)
            else:
                nc.vector.tensor_scalar(out=dst, in0=src, scalar1=factor, scalar2=0.0, op0=ALU.mult, op1=ALU.max)

        def hidden(engine, h_span, first):
            bank, width = tiles["hidden_bank", first]
            h = tile_of(("h", h_span), work, [P, 2 * h_span[1]], BF16, "h")
            lo = first - h_span[0]
            dst = h[:, 2 * lo : 2 * (lo + width)].rearrange("p (r s k) -> p r s k", s=2, k=2)
            scaled_relu(engine, dst, bank[:].rearrange("p s (r k) -> p r s k", k=2), SCALE0)

        def quantize_h(h_span):
            n = h_span[1] // 2
            codes = tile_of(("h_codes", h_span), work, [P, n], U32, "h_codes")
            scales = tile_of(("h_scales", h_span), work, [P, n], U8, "h_scales")
            nc.vector.quantize_mx(out=codes[:].bitcast(FP8X4), scales=scales[:], in_=tiles["h", h_span][:])

        def layer2_pass(dst, h_span, lo, width, t):
            w_cols = slice(t * P, (t + 1) * P)
            nc.tensor.matmul_mx(
                out=dst,
                lhsT=w1_codes[:, w_cols].bitcast(FP8X4),
                lhsT_scale=w1_scales[:, w_cols],
                rhs=tiles["h_codes", h_span][:, lo : lo + width].bitcast(FP8X4),
                rhs_scale=tiles["h_scales", h_span][:, lo : lo + width],
                start=True,
                stop=True,
            )

        def layer2(h_span):
            n = h_span[1] // 2
            width = min(n, BANK_N)
            for lo in range(0, n, width):
                bank = psum.tile([P, 2, width], F32, name="out_bank", tag="bank")
                for t in range(2):
                    layer2_pass(bank[:, t, :], h_span, lo, width, t)
                tiles["out_bank", h_span[0] + 2 * lo] = (bank, width)

        def out_rows(span):
            b, lo = divmod(span[0] // 2, R)
            return out[b].rearrange("(m t) r -> m t r", t=2)[:, :, lo : lo + span[1] // 2]

        def out_tile(span):
            b, lo = divmod(span[0] // 2, R)
            return tile_of(("out", b), outp, [P, 2, R], F32, "o_sb")[:, :, lo : lo + span[1] // 2]

        def finish(engine, span):
            scaled_relu(engine, out_tile(span), tiles["out_bank", span[0]][0][:], SCALE1)
            nc.sync.dma_start(out=out_rows(span), in_=out_tile(span))

        def finish_tile(engine, span, src, t):
            scaled_relu(engine, out_tile(span)[:, t], src, SCALE1)
            nc.sync.dma_start(out=out_rows(span)[:, t], in_=out_tile(span)[:, t])

        batch = [(b * Q, Q) for b in range(BS)]
        lower = [(b * Q, BANK_N) for b in range(BS)]
        upper = [(b * Q + BANK_N, BANK_N) for b in range(BS)]
        third, fourth = (upper[7][0], BANK_N // 2), (upper[7][0] + BANK_N // 2, BANK_N // 2)

        def hidden_batch(b):
            hidden("S", batch[b], lower[b][0])
            hidden("S", batch[b], upper[b][0])

        def first_layer(span):
            quantize_x(span)
            layer1(span)

        def second_layer(h_span):
            quantize_h(h_span)
            layer2(h_span)

        weights_after = {groups[2]: (w0_sb, w0), groups[3]: (w1_sb, w1)}
        for group in groups:
            for g in range(G):
                for b in range(group[0], group[0] + group[1]):
                    for slots in [slice(0, 1), slice(1, 2)] if b == 0 else [slice(0, 2)]:
                        load_x(b, g, slots)
            if group in weights_after:
                load_w(*weights_after[group])

        warm = keep.tile([P, 1], F32, name="warm")
        nc.vector.memset(warm[:], 0.0)
        nc.scalar.activation(out=warm[:], in_=warm[:], func=ACT.Relu)

        ident = keep.tile([P, P], F32, name="ident")
        make_identity(nc, ident[:])
        w0_banks = [transpose_weights(w0_sb, G, g) for g in range(G)]

        for g, s in ((0, 0), (0, 1), (1, 0)):
            widen("V", groups[0], g, s, 0, FIRST_SPLIT)
            widen("S", groups[0], g, s, FIRST_SPLIT)
        widen("S", groups[0], 1, 1)
        for g in range(G):
            widen("S", groups[1], g, 1)
        interleave([batch[0]], 0, 1)
        widen("V", groups[1], 0, 0)
        quantize_x(batch[0], 0, 1)
        interleave([batch[0]], 1, 2)
        widen("V", groups[1], 1, 0)
        quantize_x(batch[0], 1, 2)
        widen("V", groups[2], 0, 0)
        interleave([batch[1]])

        for g in range(G):
            widen("S", groups[2], g, 1)
        for g in range(G):
            weights_out(w0_banks[g], w0_grouped[:, g * HID * 4 : (g + 1) * HID * 4])
        w1_bank = transpose_weights(w1_sb, 1, 0)
        for g in range(G):
            widen("S", groups[3], g, 1)
        weights_out(w1_bank, w1_grouped[:])
        widen("S", groups[3], 1, 0, 0, SHARE)
        widen("V", groups[2], 1, 0)
        quantize_x(batch[1])
        widen("V", groups[3], 0, 0)
        interleave([batch[2]])
        quantize_w(w0_grouped, w0_codes, w0_scales)
        for b in range(2):
            layer1(batch[b])
            hidden_batch(b)
        first_layer(batch[2])
        interleave([batch[3]])
        widen("V", groups[3], 1, 0, SHARE)
        first_layer(batch[3])
        widen("S", groups[4], 0, 1)
        hidden_batch(2)
        widen("S", groups[4], 1, 1)
        interleave([lower[4], upper[4]])
        quantize_w(w1_grouped, w1_codes, w1_scales)
        second_layer(batch[0])
        first_layer(lower[4])
        widen("V", groups[4], 0, 0)
        first_layer(upper[4])
        finish("S", batch[0])
        interleave([lower[5], upper[5]])
        second_layer(batch[1])
        widen("V", groups[4], 1, 0)
        hidden_batch(3)
        finish("S", batch[1])
        first_layer(lower[5])
        second_layer(batch[2])
        interleave([lower[6], upper[6]])
        first_layer(upper[5])
        hidden_batch(4)
        finish("S", batch[2])
        second_layer(batch[3])

        hidden_batch(5)
        first_layer(lower[6])
        interleave([lower[7]])
        first_layer(upper[6])
        second_layer(batch[4])
        finish("S", batch[3])
        first_layer(lower[7])
        hidden_batch(6)
        interleave([third, fourth])
        second_layer(batch[5])
        finish("S", batch[4])
        finish("S", batch[5])
        first_layer(third)
        bank = psum.tile([P, 2, fourth[1]], F32, name="hidden_bank", tag="bank")
        for g in range(G):
            quantize_x(fourth, g, g + 1)
            for t in range(2):
                layer1_pass(bank[:, t, :], fourth, 0, fourth[1], t, g, (g, t) == (0, 0), (g, t) == (G - 1, 1))
        tiles["hidden_bank", fourth[0]] = (bank, fourth[1])

        second_layer(batch[6])
        hidden("V", lower[7], lower[7][0])
        hidden("V", upper[7], third[0])
        second_layer(lower[7])
        hidden("S", upper[7], fourth[0])
        for t in range(2):
            finish_tile("S", batch[6], tiles["out_bank", batch[6][0]][0][:, t, :], t)
        quantize_h(upper[7])
        finish("V", lower[7])
        for t, engine in enumerate("VS"):
            bank = psum.tile([P, upper[7][1] // 2], F32, name="last_bank", tag="bank")
            layer2_pass(bank[:], upper[7], 0, upper[7][1] // 2, t)
            finish_tile(engine, upper[7], bank[:], t)
